import numpy as np
import ml_dtypes


def mxq(x, axis, fmt="e4m3"):
    dtype, down = {"e4m3": (ml_dtypes.float8_e4m3fn, 7), "e5m2": (ml_dtypes.float8_e5m2, 14)}[fmt]
    v = np.moveaxis(np.asarray(x, np.float32).astype(ml_dtypes.bfloat16).astype(np.float64), axis, -1)
    blocks = v.reshape(v.shape[:-1] + (-1, 32))
    amax = np.abs(blocks).max(-1, keepdims=True)
    byte = np.maximum(np.where(amax > 0, np.frexp(amax)[1] - 1 + 127, 0) - down, 1)
    scale = np.exp2(byte - 127.0)
    codes = (blocks / scale).astype(np.float32).astype(dtype).astype(np.float64)
    return np.moveaxis((codes * scale).reshape(v.shape), -1, axis)


WIDE = False


def mx_kscale(k):
    if not WIDE:
        return np.ones(k)
    levels = np.array([10, -10, 5, -5, 0])
    a = np.random.permutation(np.resize(levels, k // 512 * 4)).reshape(k // 512, 4)
    idx = np.arange(k)
    return np.exp2(a[idx // 512, idx % 128 // 32])


BF16 = ml_dtypes.bfloat16


def bf(x):
    return np.asarray(x, np.float32).astype(BF16)


def f64(x):
    return np.asarray(x).astype(np.float64)


E2M1 = np.array([0.0, 0.5, 1.0, 1.5, 2.0, 3.0, 4.0, 6.0, -0.0, -0.5, -1.0, -1.5, -2.0, -3.0, -4.0, -6.0])


def pack_weight(w, fmt):
    k, n = w.shape
    w = f64(bf(w)).reshape(k // 32, 32, n)
    amax = np.abs(w).max(1)
    if fmt == "e4m3":
        byte = np.frexp(amax)[1] - 1 + 127 - 7
    else:
        mant, ex = np.frexp(amax / 6.0)
        byte = np.where(mant > 0.5, ex, ex - 1) + 127
    byte = np.clip(np.where(amax > 0, byte, 1), 1, 254)
    scaled = (w * np.exp2(127.0 - byte)[:, None, :]).reshape(k, n).astype(np.float32)
    by_word = np.ascontiguousarray(scaled.reshape(k // 512, 128, 4, n).transpose(0, 1, 3, 2))
    if fmt == "e4m3":
        words = by_word.astype(ml_dtypes.float8_e4m3fn).view(np.uint8)
    else:
        c = by_word.astype(ml_dtypes.float4_e2m1fn).view(np.uint8) & 0xF
        words = c[..., 0::2] | (c[..., 1::2] << 4)
    return np.ascontiguousarray(words), np.ascontiguousarray(byte.astype(np.uint8).reshape(k // 512, 16, n))


def unpack_weight(words, scales, fmt):
    g, p, n, _ = words.shape
    if fmt == "e4m3":
        vals = np.ascontiguousarray(words).view(ml_dtypes.float8_e4m3fn).astype(np.float64)
    else:
        nib = np.empty((g, p, n, 4), np.uint8)
        nib[..., 0::2] = words & 0xF
        nib[..., 1::2] = words >> 4
        vals = E2M1[nib]
    vals = vals * np.repeat(np.exp2(scales.astype(np.float64) - 127.0), 8, axis=1)[..., None]
    return vals.transpose(0, 1, 3, 2).reshape(g * 512, n)


B, D, DC, NREF = 512, 1024, 512, 16384
KAPPA = 1.25


def logsumexp_rows(v):
    m = v.max(axis=1, keepdims=True)
    return np.log(np.exp(v - m).sum(axis=1)) + m[:, 0]


def setup_inputs():
    s = mx_kscale(D)
    h0 = np.exp(-2.0 * KAPPA / np.sqrt(DC)) / np.sqrt(2.0 * np.pi)
    sig = h0 * np.sqrt(2.0 * KAPPA) / DC ** 0.25
    x = bf(np.random.standard_normal((B, D)) * s)
    pca_weight = np.random.standard_normal((DC, D)) * 0.95 * sig / np.sqrt(D) / s[None, :]
    words, scales = pack_weight(np.ascontiguousarray(pca_weight.T), "e4m3")
    return {"x": x,
            "pca_weight_words": words,
            "pca_weight_scales": scales,
            "pca_bias": bf(np.random.standard_normal(DC) * 0.3 * sig),
            "X_ref": bf(np.random.standard_normal((NREF, DC)) * sig),
            "bandwidth": bf(h0 * np.exp(np.random.standard_normal(1) * 2.0 / DC))}


def reference(x, pca_weight_words, pca_weight_scales, pca_bias, X_ref, bandwidth):
    r = f64(X_ref)
    h = f64(bandwidth)
    z = (mxq(f64(x), 1, "e4m3") @ unpack_weight(pca_weight_words, pca_weight_scales, "e4m3")) + f64(pca_bias)
    n, d = r.shape
    d2 = (np.sum(z * z, axis=-1, keepdims=True)
          + np.sum(r * r, axis=-1)[None, :]
          - 2.0 * (mxq(z, 1, "e4m3") @ mxq(r, 1, "e4m3").T))
    d2 = np.maximum(d2, 0.0)
    coeff = -np.log(n) - np.log(2.0 * np.pi) * d / 2.0 - np.log(h) * d
    logits = d2 / (-2.0 * h * h)
    return logsumexp_rows(logits) + coeff

@@ -1,0 +1,377 @@
+import math
+from contextlib import ExitStack
+
+import concourse.masks as masks
+import concourse.mybir as mybir
+
+F32 = mybir.dt.float32
+BF16 = mybir.dt.bfloat16
+I32 = mybir.dt.int32
+U32 = mybir.dt.uint32
+U8 = mybir.dt.uint8
+FP8X4 = mybir.dt.float8_e4m3fn_x4
+ALU = mybir.AluOpType
+ACT = mybir.ActivationFunctionType
+AXIS_X = mybir.AxisListType.X
+
+P = 128
+PACK = 4
+K_PASS = P * PACK
+BANK = 512
+
+B, D, DC, NREF = 512, 1024, 512, 16384
+ROW_TILES = B // P
+X_PASSES = D // K_PASS
+CHUNK = 2048
+N_CHUNKS = NREF // CHUNK
+REF_TILES = CHUNK // P
+BANKS = CHUNK // BANK
+TILES_PER_BANK = BANK // P
+VECTOR_NORMS = 1
+
+FLOPS = 2 * B * D * DC + 2 * B * DC * NREF
+
+
+def tile_kernelloglikelihood_kernel(
+    tc, x, pca_weight_words, pca_weight_scales, pca_bias, X_ref, bandwidth, out
+):
+    nc = tc.nc
+    with ExitStack() as ctx:
+        keep = ctx.enter_context(tc.tile_pool(name="keep", bufs=1))
+        rows_pool = ctx.enter_context(tc.tile_pool(name="rows", bufs=3))
+        grouped_pool = ctx.enter_context(tc.tile_pool(name="grouped", bufs=3))
+        chunk_pool = ctx.enter_context(tc.tile_pool(name="chunk", bufs=2))
+        dist_pool = ctx.enter_context(tc.tile_pool(name="dist", bufs=4))
+        junk_pool = ctx.enter_context(tc.tile_pool(name="junk", bufs=2))
+        psum_turn = ctx.enter_context(tc.psum_pool(name="psum_turn", bufs=2))
+        psum_spread = ctx.enter_context(tc.psum_pool(name="psum_spread", bufs=1))
+        psum_prod = ctx.enter_context(tc.psum_pool(name="psum_prod", bufs=5))
+
+        w_scales = keep.tile([P, X_PASSES, DC], U8, align_bytes=64)
+        nc.vector.memset(w_scales[:].rearrange("p g n -> p (g n)").bitcast(I32), 0)
+
+        chunks = {}
+
+        def load_chunk(k):
+            rows = rows_pool.tile([P, REF_TILES, DC], BF16, tag="rows")
+            source = X_ref[k * CHUNK : (k + 1) * CHUNK, :].rearrange(
+                "(p a) c -> p a c", a=REF_TILES
+            )
+            for q in range(BANKS):
+                tiles_of_bank = slice(q * TILES_PER_BANK, (q + 1) * TILES_PER_BANK)
+                nc.sync.dma_start(out=rows[:, tiles_of_bank, :], in_=source[:, tiles_of_bank, :])
+            chunks[k] = {"rows": rows}
+
+        h_bf16 = keep.tile([P, 1], BF16)
+        nc.sync.dma_start(out=h_bf16[:], in_=bandwidth.partition_broadcast(P))
+        load_chunk(0)
+        for g in range(X_PASSES):
+            for quadrant in range(4):
+                nc.sync.dma_start(
+                    out=w_scales[32 * quadrant : 32 * quadrant + 4, g, :].bitcast(I32),
+                    in_=pca_weight_scales[g, 4 * quadrant : 4 * quadrant + 4, :].bitcast(I32),
+                )
+        x_rows = keep.tile([P, ROW_TILES, D], BF16)
+        nc.sync.dma_start(out=x_rows[:], in_=x.rearrange("(t p) k -> p t k", p=P))
+        w_codes = keep.tile([P, X_PASSES, DC], U32, align_bytes=64)
+        for g in range(X_PASSES):
+            nc.sync.dma_start(
+                out=w_codes[:, g, :].bitcast(I32),
+                in_=pca_weight_words[g].rearrange("p n t -> p (n t)").bitcast(I32),
+            )
+        bias_bc = keep.tile([P, DC], BF16)
+        nc.sync.dma_start(out=bias_bc[:], in_=pca_bias.partition_broadcast(P))
+
+        load_chunk(1)
+
+        result = keep.tile([P, P], F32)
+        nc.vector.memset(result[:], 0.0)
+
+        ident_f32 = keep.tile([P, P], F32)
+        masks.make_identity(nc, ident_f32[:])
+        ident_bf16 = keep.tile([P, P], BF16)
+        masks.make_identity(nc, ident_bf16[:])
+
+        h = keep.tile([P, 1], F32)
+        nc.vector.tensor_copy(out=h[:], in_=h_bf16[:])
+        inv_h = keep.tile([P, 1], F32)
+        nc.vector.reciprocal(out=inv_h[:], in_=h[:])
+        neg_s = keep.tile([P, 1], F32)
+        nc.vector.scalar_tensor_tensor(
+            out=neg_s[:], in0=inv_h[:], scalar=-1.0, in1=inv_h[:], op0=ALU.mult, op1=ALU.mult
+        )
+        half_s = keep.tile([P, 1], F32)
+        nc.vector.tensor_scalar(
+            out=half_s[:], in0=neg_s[:], scalar1=-0.5, scalar2=None, op0=ALU.mult
+        )
+        norm_scale = keep.tile([P, 1], F32)
+        nc.vector.tensor_scalar(
+            out=norm_scale[:], in0=inv_h[:], scalar1=math.sqrt(0.5), scalar2=None, op0=ALU.mult
+        )
+
+        x_words = x_rows[:].bitcast(F32)
+        x_grouped = keep.tile([P, X_PASSES * B * PACK], BF16, align_bytes=64)
+        x_grouped_words = x_grouped[:].bitcast(F32).rearrange(
+            "p (g i u) -> p g i u", g=X_PASSES, u=2
+        )
+        for tau in range(ROW_TILES):
+            x_turned = psum_turn.tile([P, X_PASSES, 2, P], F32, tag="turned")
+            for g in range(X_PASSES):
+                for u in range(2):
+                    nc.tensor.transpose(
+                        x_turned[:, g, u, :],
+                        x_words[:, tau, 256 * g + u : 256 * (g + 1) : 2],
+                        ident_f32[:],
+                    )
+            nc.vector.tensor_copy(
+                out=x_grouped_words[:, :, tau * P : (tau + 1) * P, :],
+                in_=x_turned[:].rearrange("p g u i -> p g i u"),
+            )
+        x_codes = keep.tile([P, X_PASSES * B], U32, align_bytes=64)
+        x_scales = keep.tile([P, X_PASSES * B], U8, align_bytes=64)
+        nc.vector.quantize_mx(
+            out=x_codes[:].bitcast(FP8X4), scales=x_scales[:], in_=x_grouped[:]
+        )
+
+        z_f32 = keep.tile([P, ROW_TILES, DC], F32)
+        z_planes = keep.tile([P, ROW_TILES, DC], BF16)
+        z_grouped = keep.tile([P, B, PACK], BF16, align_bytes=64)
+        zeta = keep.tile([P, ROW_TILES], F32)
+        for tau in range(ROW_TILES):
+            rows_of_tile = slice(tau * P, (tau + 1) * P)
+            z_acc = psum_prod.tile([P, DC], F32, tag="prod")
+            for g in range(X_PASSES):
+                lhs_cols = slice(g * B + tau * P, g * B + (tau + 1) * P)
+                nc.tensor.matmul_mx(
+                    out=z_acc[:],
+                    lhsT=x_codes[:, lhs_cols].bitcast(FP8X4),
+                    lhsT_scale=x_scales[:, lhs_cols],
+                    rhs=w_codes[:, g, :].bitcast(FP8X4),
+                    rhs_scale=w_scales[:, g, :],
+                    start=(g == 0),
+                    stop=(g == X_PASSES - 1),
+                )
+            nc.vector.tensor_tensor(
+                out=z_f32[:, tau, :], in0=z_acc[:], in1=bias_bc[:], op=ALU.add
+            )
+            z_squares = junk_pool.tile([P, DC], BF16, tag="squares")
+            nc.scalar.activation(
+                out=z_squares[:],
+                in_=z_f32[:, tau, :],
+                func=ACT.Square,
+                scale=norm_scale[:, 0:1],
+                accum_out=zeta[:, tau : tau + 1],
+            )
+            nc.vector.tensor_copy(
+                out=z_planes[:, tau, :].rearrange("i (u e p) -> i u e p", u=2, e=2),
+                in_=z_f32[:, tau, :].rearrange("i (u p e) -> i u e p", u=2, e=2),
+            )
+            z_turned = psum_turn.tile([P, PACK, P], BF16, tag="turned")
+            for t in range(PACK):
+                nc.tensor.transpose(
+                    z_turned[:, t, :], z_planes[:, tau, t * P : (t + 1) * P], ident_bf16[:]
+                )
+            nc.vector.tensor_copy(
+                out=z_grouped[:, rows_of_tile, :], in_=z_turned[:].rearrange("p t i -> p i t")
+            )
+        z_codes = keep.tile([P, B], U32, align_bytes=64)
+        z_scales = keep.tile([P, B], U8, align_bytes=64)
+        nc.vector.quantize_mx(
+            out=z_codes[:].bitcast(FP8X4),
+            scales=z_scales[:],
+            in_=z_grouped[:].rearrange("p i t -> p (i t)"),
+        )
+        neg_zeta = keep.tile([P, ROW_TILES], F32)
+        nc.vector.tensor_scalar(
+            out=neg_zeta[:], in0=zeta[:], scalar1=-1.0, scalar2=None, op0=ALU.mult
+        )
+
+        def prepare_bank(k, q):
+            chunk = chunks[k]
+            if q == 0:
+                chunk["codes"] = chunk_pool.tile(
+                    [P, CHUNK], U32, tag="codes", name="codes", align_bytes=64
+                )
+                chunk["scales"] = chunk_pool.tile(
+                    [P, CHUNK], U8, tag="scales", name="scales", align_bytes=64
+                )
+                chunk["norms_scalar"] = chunk_pool.tile(
+                    [P, REF_TILES], F32, tag="norms_scalar", name="norms_scalar"
+                )
+                chunk["norms_vector"] = chunk_pool.tile(
+                    [P, REF_TILES], F32, tag="norms_vector", name="norms_vector"
+                )
+                chunk["norms_bc"] = chunk_pool.tile(
+                    [P, CHUNK], F32, tag="norms_bc", name="norms_bc"
+                )
+            rows = chunk["rows"]
+            cols = slice(q * BANK, (q + 1) * BANK)
+            first_tile = q * TILES_PER_BANK
+
+            norms_of_tile = []
+            for a in range(first_tile, first_tile + TILES_PER_BANK):
+                if a - first_tile < TILES_PER_BANK - VECTOR_NORMS:
+                    norms = chunk["norms_scalar"]
+                    squares = junk_pool.tile([P, DC], BF16, tag="squares")
+                    nc.scalar.activation(
+                        out=squares[:],
+                        in_=rows[:, a, :],
+                        func=ACT.Square,
+                        scale=norm_scale[:, 0:1],
+                        accum_out=norms[:, a : a + 1],
+                    )
+                else:
+                    norms = chunk["norms_vector"]
+                    products = junk_pool.tile([P, DC], F32, tag="products")
+                    nc.vector.scalar_tensor_tensor(
+                        out=products[:],
+                        in0=rows[:, a, :],
+                        scalar=half_s[:, 0:1],
+                        in1=rows[:, a, :],
+                        op0=ALU.mult,
+                        op1=ALU.mult,
+                        accum_out=norms[:, a : a + 1],
+                    )
+                norms_of_tile.append(norms[:, a : a + 1])
+
+            row_words = rows[:].bitcast(F32)
+            grouped = grouped_pool.tile([P, BANK * PACK], BF16, tag="grouped", align_bytes=64)
+            grouped_words = grouped[:].bitcast(F32).rearrange(
+                "p (a j u) -> p a j u", a=TILES_PER_BANK, u=2
+            )
+            for pair in range(TILES_PER_BANK // 2):
+                turned = psum_turn.tile([P, 2, 2, P], F32, tag="turned")
+                for a2 in range(2):
+                    for u in range(2):
+                        nc.tensor.transpose(
+                            turned[:, a2, u, :],
+                            row_words[:, first_tile + 2 * pair + a2, u * P : (u + 1) * P],
+                            ident_f32[:],
+                        )
+                nc.scalar.copy(
+                    out=grouped_words[:, 2 * pair : 2 * pair + 2, :, :],
+                    in_=turned[:].rearrange("p a u j -> p a j u"),
+                )
+            nc.vector.quantize_mx(
+                out=chunk["codes"][:, cols].bitcast(FP8X4),
+                scales=chunk["scales"][:, cols],
+                in_=grouped[:],
+            )
+
+            spread = psum_spread.tile([P, TILES_PER_BANK, P], F32, tag="spread")
+            for a4 in range(TILES_PER_BANK):
+                nc.tensor.transpose(
+                    spread[:, a4, :], norms_of_tile[a4].to_broadcast([P, P]), ident_f32[:]
+                )
+            nc.scalar.copy(
+                out=chunk["norms_bc"][:, cols], in_=spread[:].rearrange("p a j -> p (a j)")
+            )
+
+        low = keep.tile([P, ROW_TILES * N_CHUNKS], F32)
+        mass = keep.tile([P, ROW_TILES * N_CHUNKS], F32)
+
+        def score(k, tau):
+            chunk = chunks[k]
+            rows_of_tile = slice(tau * P, (tau + 1) * P)
+            dist = dist_pool.tile([P, CHUNK], F32, tag="dist")
+            for q in range(BANKS):
+                cols = slice(q * BANK, (q + 1) * BANK)
+                prod = psum_prod.tile([P, BANK], F32, tag="prod")
+                nc.tensor.matmul_mx(
+                    out=prod[:],
+                    lhsT=z_codes[:, rows_of_tile].bitcast(FP8X4),
+                    lhsT_scale=z_scales[:, rows_of_tile],
+                    rhs=chunk["codes"][:, cols].bitcast(FP8X4),
+                    rhs_scale=chunk["scales"][:, cols],
+                    start=True,
+                    stop=True,
+                )
+                nc.vector.scalar_tensor_tensor(
+                    out=dist[:, cols],
+                    in0=prod[:],
+                    scalar=neg_s[:, 0:1],
+                    in1=chunk["norms_bc"][:, cols],
+                    op0=ALU.mult,
+                    op1=ALU.add,
+                )
+            here = slice(tau * N_CHUNKS + k, tau * N_CHUNKS + k + 1)
+            nc.vector.tensor_scalar(
+                out=dist[:],
+                in0=dist[:],
+                scalar1=neg_zeta[:, tau : tau + 1],
+                scalar2=None,
+                op0=ALU.max,
+                op1=ALU.min,
+                accum_out=low[:, here],
+            )
+            terms = junk_pool.tile([P, CHUNK], BF16, tag="terms")
+            nc.scalar.activation(
+                out=terms[:],
+                in_=dist[:],
+                func=ACT.Exp,
+                scale=-1.0,
+                bias=low[:, here],
+                accum_out=mass[:, here],
+            )
+
+        for q in range(BANKS):
+            prepare_bank(0, q)
+        for k in range(N_CHUNKS):
+            if k + 2 < N_CHUNKS:
+                load_chunk(k + 2)
+            for tau in range(ROW_TILES):
+                if k + 1 < N_CHUNKS:
+                    prepare_bank(k + 1, tau)
+                score(k, tau)
+
+        by_tile = "p (t k) -> p t k"
+        lowest = keep.tile([P, ROW_TILES], F32)
+        nc.vector.tensor_reduce(
+            out=lowest[:], in_=low[:].rearrange(by_tile, t=ROW_TILES), axis=AXIS_X, op=ALU.min
+        )
+        weight = keep.tile([P, ROW_TILES * N_CHUNKS], F32)
+        nc.vector.tensor_tensor(
+            out=weight[:].rearrange(by_tile, t=ROW_TILES),
+            in0=low[:].rearrange(by_tile, t=ROW_TILES),
+            in1=lowest[:].unsqueeze(2).to_broadcast([P, ROW_TILES, N_CHUNKS]),
+            op=ALU.subtract,
+        )
+        nc.scalar.activation(out=weight[:], in_=weight[:], func=ACT.Exp, scale=-1.0)
+        nc.vector.tensor_tensor(out=weight[:], in0=weight[:], in1=mass[:], op=ALU.mult)
+        total = keep.tile([P, ROW_TILES], F32)
+        nc.vector.tensor_reduce(
+            out=total[:], in_=weight[:].rearrange(by_tile, t=ROW_TILES), axis=AXIS_X, op=ALU.add
+        )
+        log_total = keep.tile([P, ROW_TILES], F32)
+        nc.scalar.activation(out=log_total[:], in_=total[:], func=ACT.Ln)
+        log_h = keep.tile([P, 1], F32)
+        nc.scalar.activation(out=log_h[:], in_=h[:], func=ACT.Ln)
+        constant = keep.tile([P, 1], F32)
+        nc.vector.tensor_scalar(
+            out=constant[:],
+            in0=log_h[:],
+            scalar1=-float(DC),
+            scalar2=-math.log(NREF) - 0.5 * DC * math.log(2.0 * math.pi),
+            op0=ALU.mult,
+            op1=ALU.add,
+        )
+        nc.vector.tensor_tensor(
+            out=result[:, 0:ROW_TILES], in0=log_total[:], in1=lowest[:], op=ALU.subtract
+        )
+        nc.vector.tensor_tensor(
+            out=result[:, 0:ROW_TILES], in0=result[:, 0:ROW_TILES], in1=zeta[:], op=ALU.subtract
+        )
+        nc.vector.tensor_scalar(
+            out=result[:, 0:ROW_TILES],
+            in0=result[:, 0:ROW_TILES],
+            scalar1=constant[:, 0:1],
+            scalar2=None,
+            op0=ALU.add,
+        )
+        result_turned = psum_turn.tile([P, P], F32, tag="turned")
+        nc.tensor.transpose(result_turned[:], result[:], ident_f32[:])
+        result_rows = keep.tile([P, P], F32)
+        nc.vector.tensor_copy(out=result_rows[:], in_=result_turned[:])
+        nc.sync.dma_start(
+            out=out.rearrange("(t p) -> t p", p=P), in_=result_rows[0:ROW_TILES, :]
+        )

@@ -22,12 +22,13 @@ BANK = 512
 B, D, DC, NREF = 512, 1024, 512, 16384
 ROW_TILES = B // P
 X_PASSES = D // K_PASS
-CHUNK = 2048
-N_CHUNKS = NREF // CHUNK
-REF_TILES = CHUNK // P
-BANKS = CHUNK // BANK
-TILES_PER_BANK = BANK // P
-VECTOR_NORMS = 1
+N_BANKS = NREF // BANK
+REF_TILES = BANK // P
+CHUNK_BANKS = 4
+CHUNK = CHUNK_BANKS * BANK
+N_CHUNKS = N_BANKS // CHUNK_BANKS
+LEAD = 6
+LOADS_AHEAD = 4
 
 FLOPS = 2 * B * D * DC + 2 * B * DC * NREF
 
@@ -38,54 +39,58 @@ def tile_kernelloglikelihood_kernel(
     nc = tc.nc
     with ExitStack() as ctx:
         keep = ctx.enter_context(tc.tile_pool(name="keep", bufs=1))
-        rows_pool = ctx.enter_context(tc.tile_pool(name="rows", bufs=3))
+        rows_pool = ctx.enter_context(tc.tile_pool(name="rows", bufs=LOADS_AHEAD + 2))
         grouped_pool = ctx.enter_context(tc.tile_pool(name="grouped", bufs=3))
-        chunk_pool = ctx.enter_context(tc.tile_pool(name="chunk", bufs=2))
-        dist_pool = ctx.enter_context(tc.tile_pool(name="dist", bufs=4))
+        bank_pool = ctx.enter_context(tc.tile_pool(name="bank", bufs=LEAD + 1))
+        dist_pool = ctx.enter_context(tc.tile_pool(name="dist", bufs=2 * ROW_TILES))
         junk_pool = ctx.enter_context(tc.tile_pool(name="junk", bufs=2))
         psum_turn = ctx.enter_context(tc.psum_pool(name="psum_turn", bufs=2))
-        psum_spread = ctx.enter_context(tc.psum_pool(name="psum_spread", bufs=1))
-        psum_prod = ctx.enter_context(tc.psum_pool(name="psum_prod", bufs=5))
+        psum_spread = ctx.enter_context(tc.psum_pool(name="psum_spread", bufs=2))
+        psum_prod = ctx.enter_context(tc.psum_pool(name="psum_prod", bufs=4))
+        ctx.enter_context(tc.manual_schedule())
 
         w_scales = keep.tile([P, X_PASSES, DC], U8, align_bytes=64)
         nc.vector.memset(w_scales[:].rearrange("p g n -> p (g n)").bitcast(I32), 0)
+        result = keep.tile([P, P], F32)
+        nc.vector.memset(result[:], 0.0)
 
-        chunks = {}
-
-        def load_chunk(k):
-            rows = rows_pool.tile([P, REF_TILES, DC], BF16, tag="rows")
-            source = X_ref[k * CHUNK : (k + 1) * CHUNK, :].rearrange(
-                "(p a) c -> p a c", a=REF_TILES
-            )
-            for q in range(BANKS):
-                tiles_of_bank = slice(q * TILES_PER_BANK, (q + 1) * TILES_PER_BANK)
-                nc.sync.dma_start(out=rows[:, tiles_of_bank, :], in_=source[:, tiles_of_bank, :])
-            chunks[k] = {"rows": rows}
-
-        h_bf16 = keep.tile([P, 1], BF16)
-        nc.sync.dma_start(out=h_bf16[:], in_=bandwidth.partition_broadcast(P))
-        load_chunk(0)
-        for g in range(X_PASSES):
-            for quadrant in range(4):
-                nc.sync.dma_start(
-                    out=w_scales[32 * quadrant : 32 * quadrant + 4, g, :].bitcast(I32),
-                    in_=pca_weight_scales[g, 4 * quadrant : 4 * quadrant + 4, :].bitcast(I32),
-                )
         x_rows = keep.tile([P, ROW_TILES, D], BF16)
-        nc.sync.dma_start(out=x_rows[:], in_=x.rearrange("(t p) k -> p t k", p=P))
         w_codes = keep.tile([P, X_PASSES, DC], U32, align_bytes=64)
+        bias_bc = keep.tile([P, DC], BF16)
+        h_bf16 = keep.tile([P, 1], BF16)
+        banks = {}
+
+        def load_x(tau):
+            nc.sync.dma_start(out=x_rows[:, tau, :], in_=x[tau * P : (tau + 1) * P, :])
+
+        def load_bank(b):
+            rows = rows_pool.tile([P, REF_TILES, DC], BF16, tag="rows")
+            nc.sync.dma_start(
+                out=rows[:],
+                in_=X_ref[b * BANK : (b + 1) * BANK, :].rearrange("(p a) c -> p a c", a=REF_TILES),
+            )
+            banks[b] = {"rows": rows}
+
+        nc.sync.dma_start(out=h_bf16[:], in_=bandwidth.partition_broadcast(P))
+        load_x(0)
+        load_bank(0)
+        for quadrant in range(4):
+            nc.sync.dma_start(
+                out=w_scales[32 * quadrant : 32 * quadrant + 4, :, :].bitcast(I32),
+                in_=pca_weight_scales[:, 4 * quadrant : 4 * quadrant + 4, :]
+                .rearrange("g r n -> r g n")
+                .bitcast(I32),
+            )
         for g in range(X_PASSES):
             nc.sync.dma_start(
                 out=w_codes[:, g, :].bitcast(I32),
                 in_=pca_weight_words[g].rearrange("p n t -> p (n t)").bitcast(I32),
             )
-        bias_bc = keep.tile([P, DC], BF16)
         nc.sync.dma_start(out=bias_bc[:], in_=pca_bias.partition_broadcast(P))
-
-        load_chunk(1)
-
-        result = keep.tile([P, P], F32)
-        nc.vector.memset(result[:], 0.0)
+        for tau in range(1, ROW_TILES):
+            load_x(tau)
+            load_bank(tau)
+        assert LOADS_AHEAD == ROW_TILES
 
         ident_f32 = keep.tile([P, P], F32)
         masks.make_identity(nc, ident_f32[:])
@@ -108,14 +113,23 @@ def tile_kernelloglikelihood_kernel(
         nc.vector.tensor_scalar(
             out=norm_scale[:], in0=inv_h[:], scalar1=math.sqrt(0.5), scalar2=None, op0=ALU.mult
         )
+        log_h = keep.tile([P, 1], F32)
+        nc.scalar.activation(out=log_h[:], in_=h[:], func=ACT.Ln)
 
         x_words = x_rows[:].bitcast(F32)
-        x_grouped = keep.tile([P, X_PASSES * B * PACK], BF16, align_bytes=64)
-        x_grouped_words = x_grouped[:].bitcast(F32).rearrange(
-            "p (g i u) -> p g i u", g=X_PASSES, u=2
-        )
-        for tau in range(ROW_TILES):
-            x_turned = psum_turn.tile([P, X_PASSES, 2, P], F32, tag="turned")
+        x_grouped = keep.tile([P, ROW_TILES, X_PASSES * P * PACK], BF16, align_bytes=64)
+        x_codes = keep.tile([P, ROW_TILES, X_PASSES * P], U32, align_bytes=64)
+        x_scales = keep.tile([P, ROW_TILES, X_PASSES * P], U8, align_bytes=64)
+        z_f32 = keep.tile([P, ROW_TILES, DC], F32)
+        z_planes = keep.tile([P, ROW_TILES, DC], BF16)
+        z_grouped = keep.tile([P, ROW_TILES, P * PACK], BF16, align_bytes=64)
+        z_codes = keep.tile([P, ROW_TILES, P], U32, align_bytes=64)
+        z_scales = keep.tile([P, ROW_TILES, P], U8, align_bytes=64)
+        zeta = keep.tile([P, ROW_TILES], F32)
+        neg_zeta = keep.tile([P, ROW_TILES], F32)
+
+        def quantise_x(tau):
+            x_turned = psum_prod.tile([P, X_PASSES, 2, P], F32, tag="prod")
             for g in range(X_PASSES):
                 for u in range(2):
                     nc.tensor.transpose(
@@ -124,28 +138,24 @@ def tile_kernelloglikelihood_kernel(
                         ident_f32[:],
                     )
             nc.vector.tensor_copy(
-                out=x_grouped_words[:, :, tau * P : (tau + 1) * P, :],
+                out=x_grouped[:, tau, :]
+                .bitcast(F32)
+                .rearrange("p (g i u) -> p g i u", g=X_PASSES, u=2),
                 in_=x_turned[:].rearrange("p g u i -> p g i u"),
             )
-        x_codes = keep.tile([P, X_PASSES * B], U32, align_bytes=64)
-        x_scales = keep.tile([P, X_PASSES * B], U8, align_bytes=64)
-        nc.vector.quantize_mx(
-            out=x_codes[:].bitcast(FP8X4), scales=x_scales[:], in_=x_grouped[:]
-        )
+            nc.vector.quantize_mx(
+                out=x_codes[:, tau, :].bitcast(FP8X4),
+                scales=x_scales[:, tau, :],
+                in_=x_grouped[:, tau, :],
+            )
 
-        z_f32 = keep.tile([P, ROW_TILES, DC], F32)
-        z_planes = keep.tile([P, ROW_TILES, DC], BF16)
-        z_grouped = keep.tile([P, B, PACK], BF16, align_bytes=64)
-        zeta = keep.tile([P, ROW_TILES], F32)
-        for tau in range(ROW_TILES):
-            rows_of_tile = slice(tau * P, (tau + 1) * P)
+        def project(tau):
             z_acc = psum_prod.tile([P, DC], F32, tag="prod")
             for g in range(X_PASSES):
-                lhs_cols = slice(g * B + tau * P, g * B + (tau + 1) * P)
                 nc.tensor.matmul_mx(
                     out=z_acc[:],
-                    lhsT=x_codes[:, lhs_cols].bitcast(FP8X4),
-                    lhsT_scale=x_scales[:, lhs_cols],
+                    lhsT=x_codes[:, tau, g * P : (g + 1) * P].bitcast(FP8X4),
+                    lhsT_scale=x_scales[:, tau, g * P : (g + 1) * P],
                     rhs=w_codes[:, g, :].bitcast(FP8X4),
                     rhs_scale=w_scales[:, g, :],
                     start=(g == 0),
@@ -154,175 +164,203 @@ def tile_kernelloglikelihood_kernel(
             nc.vector.tensor_tensor(
                 out=z_f32[:, tau, :], in0=z_acc[:], in1=bias_bc[:], op=ALU.add
             )
-            z_squares = junk_pool.tile([P, DC], BF16, tag="squares")
-            nc.scalar.activation(
-                out=z_squares[:],
-                in_=z_f32[:, tau, :],
-                func=ACT.Square,
-                scale=norm_scale[:, 0:1],
-                accum_out=zeta[:, tau : tau + 1],
-            )
             nc.vector.tensor_copy(
                 out=z_planes[:, tau, :].rearrange("i (u e p) -> i u e p", u=2, e=2),
                 in_=z_f32[:, tau, :].rearrange("i (u p e) -> i u e p", u=2, e=2),
             )
-            z_turned = psum_turn.tile([P, PACK, P], BF16, tag="turned")
+            z_products = junk_pool.tile([P, DC], F32, tag="z_products")
+            nc.vector.scalar_tensor_tensor(
+                out=z_products[:],
+                in0=z_f32[:, tau, :],
+                scalar=half_s[:, 0:1],
+                in1=z_f32[:, tau, :],
+                op0=ALU.mult,
+                op1=ALU.mult,
+                accum_out=zeta[:, tau : tau + 1],
+            )
+            nc.vector.tensor_scalar(
+                out=neg_zeta[:, tau : tau + 1],
+                in0=zeta[:, tau : tau + 1],
+                scalar1=-1.0,
+                scalar2=None,
+                op0=ALU.mult,
+            )
+
+        def quantise_z(tau):
+            z_turned = psum_prod.tile([P, PACK, P], BF16, tag="prod")
             for t in range(PACK):
                 nc.tensor.transpose(
                     z_turned[:, t, :], z_planes[:, tau, t * P : (t + 1) * P], ident_bf16[:]
                 )
             nc.vector.tensor_copy(
-                out=z_grouped[:, rows_of_tile, :], in_=z_turned[:].rearrange("p t i -> p i t")
+                out=z_grouped[:, tau, :].rearrange("p (i t) -> p i t", t=PACK),
+                in_=z_turned[:].rearrange("p t i -> p i t"),
             )
-        z_codes = keep.tile([P, B], U32, align_bytes=64)
-        z_scales = keep.tile([P, B], U8, align_bytes=64)
-        nc.vector.quantize_mx(
-            out=z_codes[:].bitcast(FP8X4),
-            scales=z_scales[:],
-            in_=z_grouped[:].rearrange("p i t -> p (i t)"),
-        )
-        neg_zeta = keep.tile([P, ROW_TILES], F32)
-        nc.vector.tensor_scalar(
-            out=neg_zeta[:], in0=zeta[:], scalar1=-1.0, scalar2=None, op0=ALU.mult
-        )
-
-        def prepare_bank(k, q):
-            chunk = chunks[k]
-            if q == 0:
-                chunk["codes"] = chunk_pool.tile(
-                    [P, CHUNK], U32, tag="codes", name="codes", align_bytes=64
-                )
-                chunk["scales"] = chunk_pool.tile(
-                    [P, CHUNK], U8, tag="scales", name="scales", align_bytes=64
-                )
-                chunk["norms_scalar"] = chunk_pool.tile(
-                    [P, REF_TILES], F32, tag="norms_scalar", name="norms_scalar"
-                )
-                chunk["norms_vector"] = chunk_pool.tile(
-                    [P, REF_TILES], F32, tag="norms_vector", name="norms_vector"
-                )
-                chunk["norms_bc"] = chunk_pool.tile(
-                    [P, CHUNK], F32, tag="norms_bc", name="norms_bc"
-                )
-            rows = chunk["rows"]
-            cols = slice(q * BANK, (q + 1) * BANK)
-            first_tile = q * TILES_PER_BANK
-
-            norms_of_tile = []
-            for a in range(first_tile, first_tile + TILES_PER_BANK):
-                if a - first_tile < TILES_PER_BANK - VECTOR_NORMS:
-                    norms = chunk["norms_scalar"]
-                    squares = junk_pool.tile([P, DC], BF16, tag="squares")
-                    nc.scalar.activation(
-                        out=squares[:],
-                        in_=rows[:, a, :],
-                        func=ACT.Square,
-                        scale=norm_scale[:, 0:1],
-                        accum_out=norms[:, a : a + 1],
-                    )
-                else:
-                    norms = chunk["norms_vector"]
-                    products = junk_pool.tile([P, DC], F32, tag="products")
-                    nc.vector.scalar_tensor_tensor(
-                        out=products[:],
-                        in0=rows[:, a, :],
-                        scalar=half_s[:, 0:1],
-                        in1=rows[:, a, :],
-                        op0=ALU.mult,
-                        op1=ALU.mult,
-                        accum_out=norms[:, a : a + 1],
-                    )
-                norms_of_tile.append(norms[:, a : a + 1])
-
-            row_words = rows[:].bitcast(F32)
-            grouped = grouped_pool.tile([P, BANK * PACK], BF16, tag="grouped", align_bytes=64)
-            grouped_words = grouped[:].bitcast(F32).rearrange(
-                "p (a j u) -> p a j u", a=TILES_PER_BANK, u=2
+            nc.vector.quantize_mx(
+                out=z_codes[:, tau, :].bitcast(FP8X4),
+                scales=z_scales[:, tau, :],
+                in_=z_grouped[:, tau, :],
             )
-            for pair in range(TILES_PER_BANK // 2):
+
+        def turn(b):
+            row_words = banks[b]["rows"][:].bitcast(F32)
+            banks[b]["turned"] = []
+            for pair in range(REF_TILES // 2):
                 turned = psum_turn.tile([P, 2, 2, P], F32, tag="turned")
                 for a2 in range(2):
                     for u in range(2):
                         nc.tensor.transpose(
                             turned[:, a2, u, :],
-                            row_words[:, first_tile + 2 * pair + a2, u * P : (u + 1) * P],
+                            row_words[:, 2 * pair + a2, u * P : (u + 1) * P],
                             ident_f32[:],
                         )
+                banks[b]["turned"].append(turned)
+
+        def norms(b):
+            norm_cols = bank_pool.tile([P, REF_TILES], F32, tag="norm_cols")
+            for a in range(REF_TILES):
+                squares = junk_pool.tile([P, DC], BF16, tag="squares")
+                nc.scalar.activation(
+                    out=squares[:],
+                    in_=banks[b]["rows"][:, a, :],
+                    func=ACT.Square,
+                    scale=norm_scale[:, 0:1],
+                    accum_out=norm_cols[:, a : a + 1],
+                )
+            banks[b]["norm_cols"] = norm_cols
+
+        def group(b):
+            grouped = grouped_pool.tile([P, BANK * PACK], BF16, tag="grouped", align_bytes=64)
+            grouped_words = grouped[:].bitcast(F32).rearrange(
+                "p (a j u) -> p a j u", a=REF_TILES, u=2
+            )
+            for pair in range(REF_TILES // 2):
                 nc.scalar.copy(
                     out=grouped_words[:, 2 * pair : 2 * pair + 2, :, :],
-                    in_=turned[:].rearrange("p a u j -> p a j u"),
+                    in_=banks[b]["turned"][pair][:].rearrange("p a u j -> p a j u"),
                 )
-            nc.vector.quantize_mx(
-                out=chunk["codes"][:, cols].bitcast(FP8X4),
-                scales=chunk["scales"][:, cols],
-                in_=grouped[:],
-            )
+            codes = bank_pool.tile([P, BANK], U32, tag="codes", align_bytes=64)
+            scales = bank_pool.tile([P, BANK], U8, tag="scales", align_bytes=64)
+            nc.vector.quantize_mx(out=codes[:].bitcast(FP8X4), scales=scales[:], in_=grouped[:])
+            banks[b]["codes"] = codes
+            banks[b]["scales"] = scales
 
-            spread = psum_spread.tile([P, TILES_PER_BANK, P], F32, tag="spread")
-            for a4 in range(TILES_PER_BANK):
+        def spread(b):
+            spread_norms = psum_spread.tile([P, REF_TILES, P], F32, tag="spread")
+            for a in range(REF_TILES):
                 nc.tensor.transpose(
-                    spread[:, a4, :], norms_of_tile[a4].to_broadcast([P, P]), ident_f32[:]
+                    spread_norms[:, a, :],
+                    banks[b]["norm_cols"][:, a : a + 1].to_broadcast([P, P]),
+                    ident_f32[:],
                 )
-            nc.scalar.copy(
-                out=chunk["norms_bc"][:, cols], in_=spread[:].rearrange("p a j -> p (a j)")
-            )
+            banks[b]["spread"] = spread_norms
+
+        def settle(b):
+            norm_rows = bank_pool.tile([P, BANK], F32, tag="norm_rows")
+            source = banks[b]["spread"][:].rearrange("p a j -> p (a j)")
+            if b % 2 == 0:
+                nc.vector.tensor_copy(out=norm_rows[:], in_=source)
+            else:
+                nc.scalar.copy(out=norm_rows[:], in_=source)
+            banks[b]["norm_rows"] = norm_rows
 
         low = keep.tile([P, ROW_TILES * N_CHUNKS], F32)
         mass = keep.tile([P, ROW_TILES * N_CHUNKS], F32)
+        dists = {}
 
-        def score(k, tau):
-            chunk = chunks[k]
-            rows_of_tile = slice(tau * P, (tau + 1) * P)
-            dist = dist_pool.tile([P, CHUNK], F32, tag="dist")
-            for q in range(BANKS):
-                cols = slice(q * BANK, (q + 1) * BANK)
+        def products(b):
+            banks[b]["prod"] = []
+            for tau in range(ROW_TILES):
                 prod = psum_prod.tile([P, BANK], F32, tag="prod")
                 nc.tensor.matmul_mx(
                     out=prod[:],
-                    lhsT=z_codes[:, rows_of_tile].bitcast(FP8X4),
-                    lhsT_scale=z_scales[:, rows_of_tile],
-                    rhs=chunk["codes"][:, cols].bitcast(FP8X4),
-                    rhs_scale=chunk["scales"][:, cols],
+                    lhsT=z_codes[:, tau, :].bitcast(FP8X4),
+                    lhsT_scale=z_scales[:, tau, :],
+                    rhs=banks[b]["codes"][:].bitcast(FP8X4),
+                    rhs_scale=banks[b]["scales"][:],
                     start=True,
                     stop=True,
                 )
+                banks[b]["prod"].append(prod)
+
+        def distances(b):
+            k = b // CHUNK_BANKS
+            cols = slice((b % CHUNK_BANKS) * BANK, (b % CHUNK_BANKS + 1) * BANK)
+            for tau in range(ROW_TILES):
+                if b % CHUNK_BANKS == 0:
+                    dists[k, tau] = dist_pool.tile([P, CHUNK], F32, tag="dist", name="dist")
                 nc.vector.scalar_tensor_tensor(
-                    out=dist[:, cols],
-                    in0=prod[:],
+                    out=dists[k, tau][:, cols],
+                    in0=banks[b]["prod"][tau][:],
                     scalar=neg_s[:, 0:1],
-                    in1=chunk["norms_bc"][:, cols],
+                    in1=banks[b]["norm_rows"][:],
                     op0=ALU.mult,
                     op1=ALU.add,
                 )
-            here = slice(tau * N_CHUNKS + k, tau * N_CHUNKS + k + 1)
+
+        def column_of(k, tau):
+            return slice(tau * N_CHUNKS + k, tau * N_CHUNKS + k + 1)
+
+        def clamp_and_min(k, tau):
             nc.vector.tensor_scalar(
-                out=dist[:],
-                in0=dist[:],
+                out=dists[k, tau][:],
+                in0=dists[k, tau][:],
                 scalar1=neg_zeta[:, tau : tau + 1],
                 scalar2=None,
                 op0=ALU.max,
                 op1=ALU.min,
-                accum_out=low[:, here],
+                accum_out=low[:, column_of(k, tau)],
             )
+
+        def exponentials(k, tau):
             terms = junk_pool.tile([P, CHUNK], BF16, tag="terms")
             nc.scalar.activation(
                 out=terms[:],
-                in_=dist[:],
+                in_=dists[k, tau][:],
                 func=ACT.Exp,
                 scale=-1.0,
-                bias=low[:, here],
-                accum_out=mass[:, here],
+                bias=low[:, column_of(k, tau)],
+                accum_out=mass[:, column_of(k, tau)],
             )
 
-        for q in range(BANKS):
-            prepare_bank(0, q)
-        for k in range(N_CHUNKS):
-            if k + 2 < N_CHUNKS:
-                load_chunk(k + 2)
-            for tau in range(ROW_TILES):
-                if k + 1 < N_CHUNKS:
-                    prepare_bank(k + 1, tau)
-                score(k, tau)
+        def is_bank(b):
+            return 0 <= b < N_BANKS
+
+        def is_row_tile(tau):
+            return 0 <= tau < ROW_TILES
+
+        assert LEAD >= ROW_TILES + 2
+        assert CHUNK_BANKS == ROW_TILES
+        last_finish = N_BANKS - 1 + ROW_TILES
+        for s in range(-LEAD, last_finish + 1):
+            if is_row_tile(s + LEAD):
+                quantise_x(s + LEAD)
+            if is_row_tile(s + LEAD - 1):
+                project(s + LEAD - 1)
+            if is_row_tile(s + LEAD - 2):
+                quantise_z(s + LEAD - 2)
+
+            if is_bank(s - CHUNK_BANKS):
+                exponentials((s - CHUNK_BANKS) // ROW_TILES, (s - CHUNK_BANKS) % ROW_TILES)
+            if is_bank(s):
+                distances(s)
+            if is_bank(s + 1):
+                products(s + 1)
+            if is_bank(s - CHUNK_BANKS + 1):
+                clamp_and_min(
+                    (s - CHUNK_BANKS + 1) // ROW_TILES, (s - CHUNK_BANKS + 1) % ROW_TILES
+                )
+            if is_bank(s + LEAD - 1):
+                group(s + LEAD - 1)
+            if is_bank(s + LEAD - 2):
+                settle(s + LEAD - 2)
+            if is_bank(s + LEAD):
+                turn(s + LEAD)
+                norms(s + LEAD)
+            if is_bank(s + LEAD - 1):
+                spread(s + LEAD - 1)
+            if is_bank(s + LEAD + LOADS_AHEAD):
+                load_bank(s + LEAD + LOADS_AHEAD)
 
         by_tile = "p (t k) -> p t k"
         lowest = keep.tile([P, ROW_TILES], F32)
@@ -337,15 +375,6 @@ def tile_kernelloglikelihood_kernel(
             op=ALU.subtract,
         )
         nc.scalar.activation(out=weight[:], in_=weight[:], func=ACT.Exp, scale=-1.0)
-        nc.vector.tensor_tensor(out=weight[:], in0=weight[:], in1=mass[:], op=ALU.mult)
-        total = keep.tile([P, ROW_TILES], F32)
-        nc.vector.tensor_reduce(
-            out=total[:], in_=weight[:].rearrange(by_tile, t=ROW_TILES), axis=AXIS_X, op=ALU.add
-        )
-        log_total = keep.tile([P, ROW_TILES], F32)
-        nc.scalar.activation(out=log_total[:], in_=total[:], func=ACT.Ln)
-        log_h = keep.tile([P, 1], F32)
-        nc.scalar.activation(out=log_h[:], in_=h[:], func=ACT.Ln)
         constant = keep.tile([P, 1], F32)
         nc.vector.tensor_scalar(
             out=constant[:],
@@ -355,18 +384,20 @@ def tile_kernelloglikelihood_kernel(
             op0=ALU.mult,
             op1=ALU.add,
         )
-        nc.vector.tensor_tensor(
-            out=result[:, 0:ROW_TILES], in0=log_total[:], in1=lowest[:], op=ALU.subtract
-        )
-        nc.vector.tensor_tensor(
-            out=result[:, 0:ROW_TILES], in0=result[:, 0:ROW_TILES], in1=zeta[:], op=ALU.subtract
-        )
+        offset = keep.tile([P, ROW_TILES], F32)
+        nc.vector.tensor_tensor(out=offset[:], in0=neg_zeta[:], in1=lowest[:], op=ALU.subtract)
         nc.vector.tensor_scalar(
-            out=result[:, 0:ROW_TILES],
-            in0=result[:, 0:ROW_TILES],
-            scalar1=constant[:, 0:1],
-            scalar2=None,
-            op0=ALU.add,
+            out=offset[:], in0=offset[:], scalar1=constant[:, 0:1], scalar2=None, op0=ALU.add
+        )
+        nc.vector.tensor_tensor(out=weight[:], in0=weight[:], in1=mass[:], op=ALU.mult)
+        total = keep.tile([P, ROW_TILES], F32)
+        nc.vector.tensor_reduce(
+            out=total[:], in_=weight[:].rearrange(by_tile, t=ROW_TILES), axis=AXIS_X, op=ALU.add
+        )
+        log_total = keep.tile([P, ROW_TILES], F32)
+        nc.scalar.activation(out=log_total[:], in_=total[:], func=ACT.Ln)
+        nc.vector.tensor_tensor(
+            out=result[:, 0:ROW_TILES], in0=log_total[:], in1=offset[:], op=ALU.add
         )
         result_turned = psum_turn.tile([P, P], F32, tag="turned")
         nc.tensor.transpose(result_turned[:], result[:], ident_f32[:])

@@ -229,7 +229,7 @@ def tile_kernelloglikelihood_kernel(
                 )
             banks[b]["norm_cols"] = norm_cols
 
-        def group(b):
+        def regroup(b):
             grouped = grouped_pool.tile([P, BANK * PACK], BF16, tag="grouped", align_bytes=64)
             grouped_words = grouped[:].bitcast(F32).rearrange(
                 "p (a j u) -> p a j u", a=REF_TILES, u=2
@@ -239,9 +239,14 @@ def tile_kernelloglikelihood_kernel(
                     out=grouped_words[:, 2 * pair : 2 * pair + 2, :, :],
                     in_=banks[b]["turned"][pair][:].rearrange("p a u j -> p a j u"),
                 )
+            banks[b]["grouped"] = grouped
+
+        def quantise(b):
             codes = bank_pool.tile([P, BANK], U32, tag="codes", align_bytes=64)
             scales = bank_pool.tile([P, BANK], U8, tag="scales", align_bytes=64)
-            nc.vector.quantize_mx(out=codes[:].bitcast(FP8X4), scales=scales[:], in_=grouped[:])
+            nc.vector.quantize_mx(
+                out=codes[:].bitcast(FP8X4), scales=scales[:], in_=banks[b]["grouped"][:]
+            )
             banks[b]["codes"] = codes
             banks[b]["scales"] = scales
 
@@ -340,8 +345,6 @@ def tile_kernelloglikelihood_kernel(
             if is_row_tile(s + LEAD - 2):
                 quantise_z(s + LEAD - 2)
 
-            if is_bank(s - CHUNK_BANKS):
-                exponentials((s - CHUNK_BANKS) // ROW_TILES, (s - CHUNK_BANKS) % ROW_TILES)
             if is_bank(s):
                 distances(s)
             if is_bank(s + 1):
@@ -351,9 +354,12 @@ def tile_kernelloglikelihood_kernel(
                     (s - CHUNK_BANKS + 1) // ROW_TILES, (s - CHUNK_BANKS + 1) % ROW_TILES
                 )
             if is_bank(s + LEAD - 1):
-                group(s + LEAD - 1)
+                regroup(s + LEAD - 1)
             if is_bank(s + LEAD - 2):
                 settle(s + LEAD - 2)
+                quantise(s + LEAD - 2)
+            if is_bank(s - CHUNK_BANKS):
+                exponentials((s - CHUNK_BANKS) // ROW_TILES, (s - CHUNK_BANKS) % ROW_TILES)
             if is_bank(s + LEAD):
                 turn(s + LEAD)
                 norms(s + LEAD)

@@ -262,11 +262,9 @@ def tile_kernelloglikelihood_kernel(
 
         def settle(b):
             norm_rows = bank_pool.tile([P, BANK], F32, tag="norm_rows")
-            source = banks[b]["spread"][:].rearrange("p a j -> p (a j)")
-            if b % 2 == 0:
-                nc.vector.tensor_copy(out=norm_rows[:], in_=source)
-            else:
-                nc.scalar.copy(out=norm_rows[:], in_=source)
+            nc.vector.tensor_copy(
+                out=norm_rows[:], in_=banks[b]["spread"][:].rearrange("p a j -> p (a j)")
+            )
             banks[b]["norm_rows"] = norm_rows
 
         low = keep.tile([P, ROW_TILES * N_CHUNKS], F32)

@@ -30,6 +30,9 @@ N_CHUNKS = N_BANKS // CHUNK_BANKS
 LEAD = 6
 LOADS_AHEAD = 4
 
+POOL_FROM = 5
+POOL_TILES = 2
+
 FLOPS = 2 * B * D * DC + 2 * B * DC * NREF
 
 
@@ -40,7 +43,8 @@ def tile_kernelloglikelihood_kernel(
     with ExitStack() as ctx:
         keep = ctx.enter_context(tc.tile_pool(name="keep", bufs=1))
         rows_pool = ctx.enter_context(tc.tile_pool(name="rows", bufs=LOADS_AHEAD + 2))
-        grouped_pool = ctx.enter_context(tc.tile_pool(name="grouped", bufs=3))
+        grouped_pool = ctx.enter_context(tc.tile_pool(name="grouped", bufs=4))
+        square_pool = ctx.enter_context(tc.tile_pool(name="square", bufs=3))
         bank_pool = ctx.enter_context(tc.tile_pool(name="bank", bufs=LEAD + 1))
         dist_pool = ctx.enter_context(tc.tile_pool(name="dist", bufs=2 * ROW_TILES))
         junk_pool = ctx.enter_context(tc.tile_pool(name="junk", bufs=2))
@@ -216,9 +220,12 @@ def tile_kernelloglikelihood_kernel(
                         )
                 banks[b]["turned"].append(turned)
 
+        def scalar_tiles(b):
+            return REF_TILES if b < POOL_FROM else REF_TILES - POOL_TILES
+
         def norms(b):
             norm_cols = bank_pool.tile([P, REF_TILES], F32, tag="norm_cols")
-            for a in range(REF_TILES):
+            for a in range(scalar_tiles(b)):
                 squares = junk_pool.tile([P, DC], BF16, tag="squares")
                 nc.scalar.activation(
                     out=squares[:],
@@ -250,21 +257,44 @@ def tile_kernelloglikelihood_kernel(
             banks[b]["codes"] = codes
             banks[b]["scales"] = scales
 
+        def squares_on_pool(b):
+            if scalar_tiles(b) == REF_TILES:
+                return
+            squares_t = square_pool.tile([P, PACK, POOL_TILES * P], F32, tag="squares_t")
+            values = banks[b]["grouped"][:].rearrange("p (a j t) -> p a t j", a=REF_TILES, t=PACK)
+            for a in range(POOL_TILES):
+                tile_values = values[:, scalar_tiles(b) + a, :, :]
+                nc.gpsimd.tensor_tensor(
+                    out=squares_t[:, :, a * P : (a + 1) * P],
+                    in0=tile_values,
+                    in1=tile_values,
+                    op=ALU.mult,
+                )
+            banks[b]["squares_t"] = squares_t
+
         def spread(b):
             spread_norms = psum_spread.tile([P, REF_TILES, P], F32, tag="spread")
-            for a in range(REF_TILES):
+            for a in range(scalar_tiles(b)):
                 nc.tensor.transpose(
                     spread_norms[:, a, :],
                     banks[b]["norm_cols"][:, a : a + 1].to_broadcast([P, P]),
                     ident_f32[:],
                 )
+            if scalar_tiles(b) < REF_TILES:
+                for t in range(PACK):
+                    nc.tensor.matmul(
+                        out=spread_norms[:, scalar_tiles(b) :, :],
+                        lhsT=half_s[:, 0:1].to_broadcast([P, P]),
+                        rhs=banks[b]["squares_t"][:, t, :],
+                        start=(t == 0),
+                        stop=(t == PACK - 1),
+                    )
             banks[b]["spread"] = spread_norms
 
         def settle(b):
             norm_rows = bank_pool.tile([P, BANK], F32, tag="norm_rows")
-            nc.vector.tensor_copy(
-                out=norm_rows[:], in_=banks[b]["spread"][:].rearrange("p a j -> p (a j)")
-            )
+            leave = nc.vector.tensor_copy if scalar_tiles(b) == REF_TILES else nc.scalar.copy
+            leave(out=norm_rows[:], in_=banks[b]["spread"][:].rearrange("p a j -> p (a j)"))
             banks[b]["norm_rows"] = norm_rows
 
         low = keep.tile([P, ROW_TILES * N_CHUNKS], F32)
@@ -353,16 +383,18 @@ def tile_kernelloglikelihood_kernel(
                 )
             if is_bank(s + LEAD - 1):
                 regroup(s + LEAD - 1)
+            if is_bank(s + 2):
+                settle(s + 2)
             if is_bank(s + LEAD - 2):
-                settle(s + LEAD - 2)
                 quantise(s + LEAD - 2)
+                squares_on_pool(s + LEAD - 2)
             if is_bank(s - CHUNK_BANKS):
                 exponentials((s - CHUNK_BANKS) // ROW_TILES, (s - CHUNK_BANKS) % ROW_TILES)
             if is_bank(s + LEAD):
                 turn(s + LEAD)
                 norms(s + LEAD)
-            if is_bank(s + LEAD - 1):
-                spread(s + LEAD - 1)
+            if is_bank(s + 3):
+                spread(s + 3)
             if is_bank(s + LEAD + LOADS_AHEAD):
                 load_bank(s + LEAD + LOADS_AHEAD)
 

@@ -30,7 +30,8 @@ N_CHUNKS = N_BANKS // CHUNK_BANKS
 LEAD = 6
 LOADS_AHEAD = 4
 
-POOL_FROM = 5
+HALF_ROOT = math.sqrt(0.5)
+POOL_FROM = 6
 POOL_TILES = 2
 
 FLOPS = 2 * B * D * DC + 2 * B * DC * NREF
@@ -55,13 +56,15 @@ def tile_kernelloglikelihood_kernel(
 
         w_scales = keep.tile([P, X_PASSES, DC], U8, align_bytes=64)
         nc.vector.memset(w_scales[:].rearrange("p g n -> p (g n)").bitcast(I32), 0)
-        result = keep.tile([P, P], F32)
-        nc.vector.memset(result[:], 0.0)
+        bias_row = keep.tile([P, DC], BF16)
+        nc.vector.memset(bias_row[:].bitcast(I32), 0)
+        h_row = keep.tile([P, 2], BF16)
+        nc.vector.memset(h_row[:].bitcast(I32), 0)
+        ones = keep.tile([P, P], BF16)
+        nc.vector.memset(ones[:], 1.0)
 
         x_rows = keep.tile([P, ROW_TILES, D], BF16)
         w_codes = keep.tile([P, X_PASSES, DC], U32, align_bytes=64)
-        bias_bc = keep.tile([P, DC], BF16)
-        h_bf16 = keep.tile([P, 1], BF16)
         banks = {}
 
         def load_x(tau):
@@ -75,9 +78,7 @@ def tile_kernelloglikelihood_kernel(
             )
             banks[b] = {"rows": rows}
 
-        nc.sync.dma_start(out=h_bf16[:], in_=bandwidth.partition_broadcast(P))
         load_x(0)
-        load_bank(0)
         for quadrant in range(4):
             nc.sync.dma_start(
                 out=w_scales[32 * quadrant : 32 * quadrant + 4, :, :].bitcast(I32),
@@ -90,35 +91,20 @@ def tile_kernelloglikelihood_kernel(
                 out=w_codes[:, g, :].bitcast(I32),
                 in_=pca_weight_words[g].rearrange("p n t -> p (n t)").bitcast(I32),
             )
-        nc.sync.dma_start(out=bias_bc[:], in_=pca_bias.partition_broadcast(P))
+        nc.sync.dma_start(out=h_row[0:1, 0:1], in_=bandwidth.unsqueeze(0))
+        nc.sync.dma_start(out=bias_row[0:1, :], in_=pca_bias.unsqueeze(0))
+        load_bank(0)
         for tau in range(1, ROW_TILES):
             load_x(tau)
             load_bank(tau)
         assert LOADS_AHEAD == ROW_TILES
 
+        half_f32 = keep.tile([P, P], F32)
+        nc.gpsimd.memset(half_f32[:], 0.5)
         ident_f32 = keep.tile([P, P], F32)
         masks.make_identity(nc, ident_f32[:])
         ident_bf16 = keep.tile([P, P], BF16)
         masks.make_identity(nc, ident_bf16[:])
-
-        h = keep.tile([P, 1], F32)
-        nc.vector.tensor_copy(out=h[:], in_=h_bf16[:])
-        inv_h = keep.tile([P, 1], F32)
-        nc.vector.reciprocal(out=inv_h[:], in_=h[:])
-        neg_s = keep.tile([P, 1], F32)
-        nc.vector.scalar_tensor_tensor(
-            out=neg_s[:], in0=inv_h[:], scalar=-1.0, in1=inv_h[:], op0=ALU.mult, op1=ALU.mult
-        )
-        half_s = keep.tile([P, 1], F32)
-        nc.vector.tensor_scalar(
-            out=half_s[:], in0=neg_s[:], scalar1=-0.5, scalar2=None, op0=ALU.mult
-        )
-        norm_scale = keep.tile([P, 1], F32)
-        nc.vector.tensor_scalar(
-            out=norm_scale[:], in0=inv_h[:], scalar1=math.sqrt(0.5), scalar2=None, op0=ALU.mult
-        )
-        log_h = keep.tile([P, 1], F32)
-        nc.scalar.activation(out=log_h[:], in_=h[:], func=ACT.Ln)
 
         x_words = x_rows[:].bitcast(F32)
         x_grouped = keep.tile([P, ROW_TILES, X_PASSES * P * PACK], BF16, align_bytes=64)
@@ -231,7 +217,7 @@ def tile_kernelloglikelihood_kernel(
                     out=squares[:],
                     in_=banks[b]["rows"][:, a, :],
                     func=ACT.Square,
-                    scale=norm_scale[:, 0:1],
+                    scale=HALF_ROOT,
                     accum_out=norm_cols[:, a : a + 1],
                 )
             banks[b]["norm_cols"] = norm_cols
@@ -284,7 +270,7 @@ def tile_kernelloglikelihood_kernel(
                 for t in range(PACK):
                     nc.tensor.matmul(
                         out=spread_norms[:, scalar_tiles(b) :, :],
-                        lhsT=half_s[:, 0:1].to_broadcast([P, P]),
+                        lhsT=half_f32[:],
                         rhs=banks[b]["squares_t"][:, t, :],
                         start=(t == 0),
                         stop=(t == PACK - 1),
@@ -293,8 +279,19 @@ def tile_kernelloglikelihood_kernel(
 
         def settle(b):
             norm_rows = bank_pool.tile([P, BANK], F32, tag="norm_rows")
-            leave = nc.vector.tensor_copy if scalar_tiles(b) == REF_TILES else nc.scalar.copy
-            leave(out=norm_rows[:], in_=banks[b]["spread"][:].rearrange("p a j -> p (a j)"))
+            spread_norms = banks[b]["spread"][:].rearrange("p a j -> p (a j)")
+            if scalar_tiles(b) == REF_TILES:
+                nc.vector.tensor_scalar(
+                    out=norm_rows[:],
+                    in0=spread_norms,
+                    scalar1=pos_s[:, 0:1],
+                    scalar2=None,
+                    op0=ALU.mult,
+                )
+            else:
+                nc.scalar.activation(
+                    out=norm_rows[:], in_=spread_norms, func=ACT.Copy, scale=pos_s[:, 0:1]
+                )
             banks[b]["norm_rows"] = norm_rows
 
         low = keep.tile([P, ROW_TILES * N_CHUNKS], F32)
@@ -356,6 +353,35 @@ def tile_kernelloglikelihood_kernel(
                 accum_out=mass[:, column_of(k, tau)],
             )
 
+        quantise_x(0)
+
+        h = keep.tile([P, 1], F32)
+        h_everywhere = psum_spread.tile([P, 2], F32, tag="spread")
+        nc.tensor.matmul(out=h_everywhere[:], lhsT=ones[:], rhs=h_row[:], start=True, stop=True)
+        nc.vector.tensor_copy(out=h[:], in_=h_everywhere[:, 0:1])
+        bias_everywhere = psum_spread.tile([P, DC], F32, tag="spread")
+        nc.tensor.matmul(
+            out=bias_everywhere[:], lhsT=ones[:], rhs=bias_row[:], start=True, stop=True
+        )
+        bias_bc = keep.tile([P, DC], F32)
+        nc.scalar.copy(out=bias_bc[:], in_=bias_everywhere[:])
+        inv_h = keep.tile([P, 1], F32)
+        nc.vector.reciprocal(out=inv_h[:], in_=h[:])
+        neg_s = keep.tile([P, 1], F32)
+        nc.vector.scalar_tensor_tensor(
+            out=neg_s[:], in0=inv_h[:], scalar=-1.0, in1=inv_h[:], op0=ALU.mult, op1=ALU.mult
+        )
+        half_s = keep.tile([P, 1], F32)
+        nc.vector.tensor_scalar(
+            out=half_s[:], in0=neg_s[:], scalar1=-0.5, scalar2=None, op0=ALU.mult
+        )
+        pos_s = keep.tile([P, 1], F32)
+        nc.vector.tensor_scalar(
+            out=pos_s[:], in0=neg_s[:], scalar1=-1.0, scalar2=None, op0=ALU.mult
+        )
+        log_h = keep.tile([P, 1], F32)
+        nc.scalar.activation(out=log_h[:], in_=h[:], func=ACT.Ln)
+
         def is_bank(b):
             return 0 <= b < N_BANKS
 
@@ -366,7 +392,7 @@ def tile_kernelloglikelihood_kernel(
         assert CHUNK_BANKS == ROW_TILES
         last_finish = N_BANKS - 1 + ROW_TILES
         for s in range(-LEAD, last_finish + 1):
-            if is_row_tile(s + LEAD):
+            if is_row_tile(s + LEAD) and s > -LEAD:
                 quantise_x(s + LEAD)
             if is_row_tile(s + LEAD - 1):
                 project(s + LEAD - 1)
@@ -432,6 +458,8 @@ def tile_kernelloglikelihood_kernel(
         )
         log_total = keep.tile([P, ROW_TILES], F32)
         nc.scalar.activation(out=log_total[:], in_=total[:], func=ACT.Ln)
+        result = keep.tile([P, P], F32)
+        nc.gpsimd.memset(result[:], 0.0)
         nc.vector.tensor_tensor(
             out=result[:, 0:ROW_TILES], in0=log_total[:], in1=offset[:], op=ALU.add
         )

@@ -115,7 +115,6 @@ def tile_kernelloglikelihood_kernel(
         z_grouped = keep.tile([P, ROW_TILES, P * PACK], BF16, align_bytes=64)
         z_codes = keep.tile([P, ROW_TILES, P], U32, align_bytes=64)
         z_scales = keep.tile([P, ROW_TILES, P], U8, align_bytes=64)
-        zeta = keep.tile([P, ROW_TILES], F32)
         neg_zeta = keep.tile([P, ROW_TILES], F32)
 
         def quantise_x(tau):
@@ -162,18 +161,11 @@ def tile_kernelloglikelihood_kernel(
             nc.vector.scalar_tensor_tensor(
                 out=z_products[:],
                 in0=z_f32[:, tau, :],
-                scalar=half_s[:, 0:1],
+                scalar=-0.5,
                 in1=z_f32[:, tau, :],
                 op0=ALU.mult,
                 op1=ALU.mult,
-                accum_out=zeta[:, tau : tau + 1],
-            )
-            nc.vector.tensor_scalar(
-                out=neg_zeta[:, tau : tau + 1],
-                in0=zeta[:, tau : tau + 1],
-                scalar1=-1.0,
-                scalar2=None,
-                op0=ALU.mult,
+                accum_out=neg_zeta[:, tau : tau + 1],
             )
 
         def quantise_z(tau):
@@ -279,22 +271,12 @@ def tile_kernelloglikelihood_kernel(
 
         def settle(b):
             norm_rows = bank_pool.tile([P, BANK], F32, tag="norm_rows")
-            spread_norms = banks[b]["spread"][:].rearrange("p a j -> p (a j)")
-            if scalar_tiles(b) == REF_TILES:
-                nc.vector.tensor_scalar(
-                    out=norm_rows[:],
-                    in0=spread_norms,
-                    scalar1=pos_s[:, 0:1],
-                    scalar2=None,
-                    op0=ALU.mult,
-                )
-            else:
-                nc.scalar.activation(
-                    out=norm_rows[:], in_=spread_norms, func=ACT.Copy, scale=pos_s[:, 0:1]
-                )
+            leave = nc.vector.tensor_copy if scalar_tiles(b) == REF_TILES else nc.scalar.copy
+            leave(out=norm_rows[:], in_=banks[b]["spread"][:].rearrange("p a j -> p (a j)"))
             banks[b]["norm_rows"] = norm_rows
 
         low = keep.tile([P, ROW_TILES * N_CHUNKS], F32)
+        low_s = keep.tile([P, ROW_TILES * N_CHUNKS], F32)
         mass = keep.tile([P, ROW_TILES * N_CHUNKS], F32)
         dists = {}
 
@@ -319,13 +301,11 @@ def tile_kernelloglikelihood_kernel(
             for tau in range(ROW_TILES):
                 if b % CHUNK_BANKS == 0:
                     dists[k, tau] = dist_pool.tile([P, CHUNK], F32, tag="dist", name="dist")
-                nc.vector.scalar_tensor_tensor(
+                nc.vector.tensor_tensor(
                     out=dists[k, tau][:, cols],
-                    in0=banks[b]["prod"][tau][:],
-                    scalar=neg_s[:, 0:1],
-                    in1=banks[b]["norm_rows"][:],
-                    op0=ALU.mult,
-                    op1=ALU.add,
+                    in0=banks[b]["norm_rows"][:],
+                    in1=banks[b]["prod"][tau][:],
+                    op=ALU.subtract,
                 )
 
         def column_of(k, tau):
@@ -341,6 +321,14 @@ def tile_kernelloglikelihood_kernel(
                 op1=ALU.min,
                 accum_out=low[:, column_of(k, tau)],
             )
+            nc.gpsimd.tensor_scalar(
+                out=low_s[:, column_of(k, tau)],
+                in0=low[:, column_of(k, tau)],
+                scalar1=pos_s[:, 0:1],
+                scalar2=0.0,
+                op0=ALU.mult,
+                op1=ALU.add,
+            )
 
         def exponentials(k, tau):
             terms = junk_pool.tile([P, CHUNK], BF16, tag="terms")
@@ -348,8 +336,8 @@ def tile_kernelloglikelihood_kernel(
                 out=terms[:],
                 in_=dists[k, tau][:],
                 func=ACT.Exp,
-                scale=-1.0,
-                bias=low[:, column_of(k, tau)],
+                scale=neg_s[:, 0:1],
+                bias=low_s[:, column_of(k, tau)],
                 accum_out=mass[:, column_of(k, tau)],
             )
 
@@ -370,10 +358,6 @@ def tile_kernelloglikelihood_kernel(
         neg_s = keep.tile([P, 1], F32)
         nc.vector.scalar_tensor_tensor(
             out=neg_s[:], in0=inv_h[:], scalar=-1.0, in1=inv_h[:], op0=ALU.mult, op1=ALU.mult
-        )
-        half_s = keep.tile([P, 1], F32)
-        nc.vector.tensor_scalar(
-            out=half_s[:], in0=neg_s[:], scalar1=-0.5, scalar2=None, op0=ALU.mult
         )
         pos_s = keep.tile([P, 1], F32)
         nc.vector.tensor_scalar(
@@ -436,7 +420,7 @@ def tile_kernelloglikelihood_kernel(
             in1=lowest[:].unsqueeze(2).to_broadcast([P, ROW_TILES, N_CHUNKS]),
             op=ALU.subtract,
         )
-        nc.scalar.activation(out=weight[:], in_=weight[:], func=ACT.Exp, scale=-1.0)
+        nc.scalar.activation(out=weight[:], in_=weight[:], func=ACT.Exp, scale=neg_s[:, 0:1])
         constant = keep.tile([P, 1], F32)
         nc.vector.tensor_scalar(
             out=constant[:],
@@ -449,7 +433,12 @@ def tile_kernelloglikelihood_kernel(
         offset = keep.tile([P, ROW_TILES], F32)
         nc.vector.tensor_tensor(out=offset[:], in0=neg_zeta[:], in1=lowest[:], op=ALU.subtract)
         nc.vector.tensor_scalar(
-            out=offset[:], in0=offset[:], scalar1=constant[:, 0:1], scalar2=None, op0=ALU.add
+            out=offset[:],
+            in0=offset[:],
+            scalar1=pos_s[:, 0:1],
+            scalar2=constant[:, 0:1],
+            op0=ALU.mult,
+            op1=ALU.add,
         )
         nc.vector.tensor_tensor(out=weight[:], in0=weight[:], in1=mass[:], op=ALU.mult)
         total = keep.tile([P, ROW_TILES], F32)

@@ -32,6 +32,8 @@ LOADS_AHEAD = 4
 
 HALF_ROOT = math.sqrt(0.5)
 POOL_FROM = 6
+VECTOR_SETTLES = 2
+TREE_LEFT = 64
 POOL_TILES = 2
 
 FLOPS = 2 * B * D * DC + 2 * B * DC * NREF
@@ -45,6 +47,7 @@ def tile_kernelloglikelihood_kernel(
         keep = ctx.enter_context(tc.tile_pool(name="keep", bufs=1))
         rows_pool = ctx.enter_context(tc.tile_pool(name="rows", bufs=LOADS_AHEAD + 2))
         grouped_pool = ctx.enter_context(tc.tile_pool(name="grouped", bufs=4))
+        tree_pool = ctx.enter_context(tc.tile_pool(name="tree", bufs=4))
         square_pool = ctx.enter_context(tc.tile_pool(name="square", bufs=3))
         bank_pool = ctx.enter_context(tc.tile_pool(name="bank", bufs=LEAD + 1))
         dist_pool = ctx.enter_context(tc.tile_pool(name="dist", bufs=2 * ROW_TILES))
@@ -93,10 +96,10 @@ def tile_kernelloglikelihood_kernel(
             )
         nc.sync.dma_start(out=h_row[0:1, 0:1], in_=bandwidth.unsqueeze(0))
         nc.sync.dma_start(out=bias_row[0:1, :], in_=pca_bias.unsqueeze(0))
-        load_bank(0)
         for tau in range(1, ROW_TILES):
             load_x(tau)
-            load_bank(tau)
+            load_bank(tau - 1)
+        load_bank(ROW_TILES - 1)
         assert LOADS_AHEAD == ROW_TILES
 
         half_f32 = keep.tile([P, P], F32)
@@ -117,7 +120,9 @@ def tile_kernelloglikelihood_kernel(
         z_scales = keep.tile([P, ROW_TILES, P], U8, align_bytes=64)
         neg_zeta = keep.tile([P, ROW_TILES], F32)
 
-        def quantise_x(tau):
+        x_turned_tiles, z_acc_tiles, z_turned_tiles = {}, {}, {}
+
+        def turn_x(tau):
             x_turned = psum_prod.tile([P, X_PASSES, 2, P], F32, tag="prod")
             for g in range(X_PASSES):
                 for u in range(2):
@@ -126,12 +131,18 @@ def tile_kernelloglikelihood_kernel(
                         x_words[:, tau, 256 * g + u : 256 * (g + 1) : 2],
                         ident_f32[:],
                     )
+            x_turned_tiles[tau] = x_turned
+
+        def regroup_x(tau):
+            x_turned = x_turned_tiles[tau]
             nc.vector.tensor_copy(
                 out=x_grouped[:, tau, :]
                 .bitcast(F32)
                 .rearrange("p (g i u) -> p g i u", g=X_PASSES, u=2),
                 in_=x_turned[:].rearrange("p g u i -> p g i u"),
             )
+
+        def quantise_x(tau):
             nc.vector.quantize_mx(
                 out=x_codes[:, tau, :].bitcast(FP8X4),
                 scales=x_scales[:, tau, :],
@@ -140,6 +151,7 @@ def tile_kernelloglikelihood_kernel(
 
         def project(tau):
             z_acc = psum_prod.tile([P, DC], F32, tag="prod")
+            z_acc_tiles[tau] = z_acc
             for g in range(X_PASSES):
                 nc.tensor.matmul_mx(
                     out=z_acc[:],
@@ -150,13 +162,19 @@ def tile_kernelloglikelihood_kernel(
                     start=(g == 0),
                     stop=(g == X_PASSES - 1),
                 )
+
+        def add_bias(tau):
             nc.vector.tensor_tensor(
-                out=z_f32[:, tau, :], in0=z_acc[:], in1=bias_bc[:], op=ALU.add
+                out=z_f32[:, tau, :], in0=z_acc_tiles[tau][:], in1=bias_bc[:], op=ALU.add
             )
+
+        def round_z(tau):
             nc.vector.tensor_copy(
                 out=z_planes[:, tau, :].rearrange("i (u e p) -> i u e p", u=2, e=2),
                 in_=z_f32[:, tau, :].rearrange("i (u p e) -> i u e p", u=2, e=2),
             )
+
+        def norm_z(tau):
             z_products = junk_pool.tile([P, DC], F32, tag="z_products")
             nc.vector.scalar_tensor_tensor(
                 out=z_products[:],
@@ -168,21 +186,30 @@ def tile_kernelloglikelihood_kernel(
                 accum_out=neg_zeta[:, tau : tau + 1],
             )
 
-        def quantise_z(tau):
+        def turn_z(tau):
             z_turned = psum_prod.tile([P, PACK, P], BF16, tag="prod")
             for t in range(PACK):
                 nc.tensor.transpose(
                     z_turned[:, t, :], z_planes[:, tau, t * P : (t + 1) * P], ident_bf16[:]
                 )
+            z_turned_tiles[tau] = z_turned
+
+        def regroup_z(tau):
+            z_turned = z_turned_tiles[tau]
             nc.vector.tensor_copy(
                 out=z_grouped[:, tau, :].rearrange("p (i t) -> p i t", t=PACK),
                 in_=z_turned[:].rearrange("p t i -> p i t"),
             )
+
+        def quantise_z(tau):
             nc.vector.quantize_mx(
                 out=z_codes[:, tau, :].bitcast(FP8X4),
                 scales=z_scales[:, tau, :],
                 in_=z_grouped[:, tau, :],
             )
+
+        def is_bank(b):
+            return 0 <= b < N_BANKS
 
         def turn(b):
             row_words = banks[b]["rows"][:].bitcast(F32)
@@ -199,11 +226,38 @@ def tile_kernelloglikelihood_kernel(
                 banks[b]["turned"].append(turned)
 
         def scalar_tiles(b):
-            return REF_TILES if b < POOL_FROM else REF_TILES - POOL_TILES
+            return REF_TILES - POOL_TILES if b >= POOL_FROM else REF_TILES
+
+        def tree_tiles(b):
+            return range(REF_TILES - 1, REF_TILES) if b < POOL_FROM else range(0)
+
+        def trees(b):
+            for a in tree_tiles(b):
+                tree = tree_pool.tile([P, DC], F32, tag="tree")
+                rows = banks[b]["rows"][:, a, :]
+                nc.gpsimd.tensor_tensor(out=tree[:], in0=rows, in1=rows, op=ALU.mult)
+                left = DC // 2
+                while left >= TREE_LEFT:
+                    nc.gpsimd.tensor_tensor(
+                        out=tree[:, 0:left], in0=tree[:, 0:left], in1=tree[:, left : 2 * left], op=ALU.add
+                    )
+                    left = left // 2
+                banks[b]["tree", a] = tree
+
+        def finish_trees(b):
+            for a in tree_tiles(b):
+                sums = junk_pool.tile([P, TREE_LEFT], F32, tag="sums")
+                nc.scalar.activation(
+                    out=sums[:],
+                    in_=banks[b]["tree", a][:, 0:TREE_LEFT],
+                    func=ACT.Copy,
+                    scale=0.5,
+                    accum_out=banks[b]["norm_cols"][:, a : a + 1],
+                )
 
         def norms(b):
             norm_cols = bank_pool.tile([P, REF_TILES], F32, tag="norm_cols")
-            for a in range(scalar_tiles(b)):
+            for a in range(scalar_tiles(b) - len(tree_tiles(b))):
                 squares = junk_pool.tile([P, DC], BF16, tag="squares")
                 nc.scalar.activation(
                     out=squares[:],
@@ -271,7 +325,7 @@ def tile_kernelloglikelihood_kernel(
 
         def settle(b):
             norm_rows = bank_pool.tile([P, BANK], F32, tag="norm_rows")
-            leave = nc.vector.tensor_copy if scalar_tiles(b) == REF_TILES else nc.scalar.copy
+            leave = nc.vector.tensor_copy if b < VECTOR_SETTLES else nc.scalar.copy
             leave(out=norm_rows[:], in_=banks[b]["spread"][:].rearrange("p a j -> p (a j)"))
             banks[b]["norm_rows"] = norm_rows
 
@@ -341,6 +395,8 @@ def tile_kernelloglikelihood_kernel(
                 accum_out=mass[:, column_of(k, tau)],
             )
 
+        turn_x(0)
+        regroup_x(0)
         quantise_x(0)
 
         h = keep.tile([P, 1], F32)
@@ -366,9 +422,8 @@ def tile_kernelloglikelihood_kernel(
         log_h = keep.tile([P, 1], F32)
         nc.scalar.activation(out=log_h[:], in_=h[:], func=ACT.Ln)
 
-        def is_bank(b):
-            return 0 <= b < N_BANKS
-
+        project(0)
+        turn_x(1)
         def is_row_tile(tau):
             return 0 <= tau < ROW_TILES
 
@@ -376,12 +431,25 @@ def tile_kernelloglikelihood_kernel(
         assert CHUNK_BANKS == ROW_TILES
         last_finish = N_BANKS - 1 + ROW_TILES
         for s in range(-LEAD, last_finish + 1):
-            if is_row_tile(s + LEAD) and s > -LEAD:
-                quantise_x(s + LEAD)
-            if is_row_tile(s + LEAD - 1):
-                project(s + LEAD - 1)
-            if is_row_tile(s + LEAD - 2):
-                quantise_z(s + LEAD - 2)
+            n = s + LEAD
+            if is_row_tile(n + 1):
+                regroup_x(n + 1)
+            if is_row_tile(n):
+                add_bias(n)
+            if is_row_tile(n - 1):
+                regroup_z(n - 1)
+            if is_row_tile(n + 2):
+                turn_x(n + 2)
+            if is_row_tile(n + 1):
+                quantise_x(n + 1)
+            if is_row_tile(n):
+                round_z(n)
+            if is_row_tile(n + 1):
+                project(n + 1)
+            if is_row_tile(n - 1):
+                quantise_z(n - 1)
+            if is_row_tile(n):
+                norm_z(n)
 
             if is_bank(s):
                 distances(s)
@@ -400,11 +468,16 @@ def tile_kernelloglikelihood_kernel(
                 squares_on_pool(s + LEAD - 2)
             if is_bank(s - CHUNK_BANKS):
                 exponentials((s - CHUNK_BANKS) // ROW_TILES, (s - CHUNK_BANKS) % ROW_TILES)
+            if is_bank(s + 3):
+                spread(s + 3)
             if is_bank(s + LEAD):
                 turn(s + LEAD)
                 norms(s + LEAD)
-            if is_bank(s + 3):
-                spread(s + 3)
+                trees(s + LEAD)
+            if is_bank(s + LEAD - 1):
+                finish_trees(s + LEAD - 1)
+            if is_row_tile(n):
+                turn_z(n)
             if is_bank(s + LEAD + LOADS_AHEAD):
                 load_bank(s + LEAD + LOADS_AHEAD)
 

@@ -32,8 +32,7 @@ LOADS_AHEAD = 4
 
 HALF_ROOT = math.sqrt(0.5)
 POOL_FROM = 6
-VECTOR_SETTLES = 2
-TREE_LEFT = 64
+VECTOR_SETTLES = 4
 POOL_TILES = 2
 
 FLOPS = 2 * B * D * DC + 2 * B * DC * NREF
@@ -47,7 +46,6 @@ def tile_kernelloglikelihood_kernel(
         keep = ctx.enter_context(tc.tile_pool(name="keep", bufs=1))
         rows_pool = ctx.enter_context(tc.tile_pool(name="rows", bufs=LOADS_AHEAD + 2))
         grouped_pool = ctx.enter_context(tc.tile_pool(name="grouped", bufs=4))
-        tree_pool = ctx.enter_context(tc.tile_pool(name="tree", bufs=4))
         square_pool = ctx.enter_context(tc.tile_pool(name="square", bufs=3))
         bank_pool = ctx.enter_context(tc.tile_pool(name="bank", bufs=LEAD + 1))
         dist_pool = ctx.enter_context(tc.tile_pool(name="dist", bufs=2 * ROW_TILES))
@@ -228,36 +226,9 @@ def tile_kernelloglikelihood_kernel(
         def scalar_tiles(b):
             return REF_TILES - POOL_TILES if b >= POOL_FROM else REF_TILES
 
-        def tree_tiles(b):
-            return range(REF_TILES - 1, REF_TILES) if b < POOL_FROM else range(0)
-
-        def trees(b):
-            for a in tree_tiles(b):
-                tree = tree_pool.tile([P, DC], F32, tag="tree")
-                rows = banks[b]["rows"][:, a, :]
-                nc.gpsimd.tensor_tensor(out=tree[:], in0=rows, in1=rows, op=ALU.mult)
-                left = DC // 2
-                while left >= TREE_LEFT:
-                    nc.gpsimd.tensor_tensor(
-                        out=tree[:, 0:left], in0=tree[:, 0:left], in1=tree[:, left : 2 * left], op=ALU.add
-                    )
-                    left = left // 2
-                banks[b]["tree", a] = tree
-
-        def finish_trees(b):
-            for a in tree_tiles(b):
-                sums = junk_pool.tile([P, TREE_LEFT], F32, tag="sums")
-                nc.scalar.activation(
-                    out=sums[:],
-                    in_=banks[b]["tree", a][:, 0:TREE_LEFT],
-                    func=ACT.Copy,
-                    scale=0.5,
-                    accum_out=banks[b]["norm_cols"][:, a : a + 1],
-                )
-
         def norms(b):
             norm_cols = bank_pool.tile([P, REF_TILES], F32, tag="norm_cols")
-            for a in range(scalar_tiles(b) - len(tree_tiles(b))):
+            for a in range(scalar_tiles(b)):
                 squares = junk_pool.tile([P, DC], BF16, tag="squares")
                 nc.scalar.activation(
                     out=squares[:],
@@ -473,9 +444,6 @@ def tile_kernelloglikelihood_kernel(
             if is_bank(s + LEAD):
                 turn(s + LEAD)
                 norms(s + LEAD)
-                trees(s + LEAD)
-            if is_bank(s + LEAD - 1):
-                finish_trees(s + LEAD - 1)
             if is_row_tile(n):
                 turn_z(n)
             if is_bank(s + LEAD + LOADS_AHEAD):

@@ -31,6 +31,9 @@ LEAD = 6
 LOADS_AHEAD = 4
 
 HALF_ROOT = math.sqrt(0.5)
+FLIP_FROM = 30
+FLIP_BANKS = N_BANKS - FLIP_FROM
+FD = 2
 POOL_FROM = 6
 VECTOR_SETTLES = 4
 POOL_TILES = 2
@@ -46,6 +49,7 @@ def tile_kernelloglikelihood_kernel(
         keep = ctx.enter_context(tc.tile_pool(name="keep", bufs=1))
         rows_pool = ctx.enter_context(tc.tile_pool(name="rows", bufs=LOADS_AHEAD + 2))
         grouped_pool = ctx.enter_context(tc.tile_pool(name="grouped", bufs=4))
+        flat_pool = ctx.enter_context(tc.tile_pool(name="flat", bufs=FLIP_BANKS * REF_TILES))
         square_pool = ctx.enter_context(tc.tile_pool(name="square", bufs=3))
         bank_pool = ctx.enter_context(tc.tile_pool(name="bank", bufs=LEAD + 1))
         dist_pool = ctx.enter_context(tc.tile_pool(name="dist", bufs=2 * ROW_TILES))
@@ -333,6 +337,93 @@ def tile_kernelloglikelihood_kernel(
                     op=ALU.subtract,
                 )
 
+        def flip(b, part):
+            for a in part:
+                flipped = psum_turn.tile([P, BANK], F32, tag="turned", name="flipped")
+                nc.tensor.matmul_mx(
+                    out=flipped[:],
+                    lhsT=banks[b]["codes"][:, a * P : (a + 1) * P].bitcast(FP8X4),
+                    lhsT_scale=banks[b]["scales"][:, a * P : (a + 1) * P],
+                    rhs=z_codes[:].rearrange("p t i -> p (t i)").bitcast(FP8X4),
+                    rhs_scale=z_scales[:].rearrange("p t i -> p (t i)"),
+                    start=True,
+                    stop=True,
+                )
+                banks[b]["flipped", a] = flipped
+
+        def flip_norms(b):
+            pool_norms = psum_spread.tile([P, POOL_TILES], F32, tag="spread", name="pool_norms")
+            for a in range(POOL_TILES):
+                for t in range(PACK):
+                    nc.tensor.matmul(
+                        out=pool_norms[:, a : a + 1],
+                        lhsT=banks[b]["squares_t"][:, t, a * P : (a + 1) * P],
+                        rhs=half_f32[:, 0:1],
+                        start=(t == 0),
+                        stop=(t == PACK - 1),
+                    )
+            banks[b]["pool_norms"] = pool_norms
+
+        def join_norms(b):
+            nc.scalar.copy(
+                out=banks[b]["norm_cols"][:, scalar_tiles(b) :], in_=banks[b]["pool_norms"][:]
+            )
+
+        def flat_distances(b, part):
+            for a in part:
+                flat = flat_pool.tile([P, BANK], F32, tag="flat", name="flat")
+                nc.scalar.activation(
+                    out=flat[:],
+                    in_=banks[b]["flipped", a][:],
+                    func=ACT.Identity,
+                    scale=-1.0,
+                    bias=banks[b]["norm_cols"][:, a : a + 1],
+                )
+                banks[b]["flat", a] = flat
+
+        flip_lows = keep.tile([P, ROW_TILES, FLIP_BANKS + 1], F32)
+        last = N_BANKS // CHUNK_BANKS - 1
+        plain_banks = CHUNK_BANKS - FLIP_BANKS
+        backs = {}
+
+        def flip_back(tau):
+            for b in range(FLIP_FROM, N_BANKS):
+                back = psum_prod.tile([P, REF_TILES, P], F32, tag="prod", name="back")
+                for a in range(REF_TILES):
+                    nc.tensor.transpose(
+                        back[:, a, :],
+                        banks[b]["flat", a][:, tau * P : (tau + 1) * P],
+                        ident_f32[:],
+                    )
+                backs[b, tau] = back
+
+        def clamp_flipped(tau):
+            clamped = dists[last, tau]
+            pieces = [(clamped[:, 0 : plain_banks * BANK], clamped[:, 0 : plain_banks * BANK])]
+            for b in range(FLIP_FROM, N_BANKS):
+                o = (b % CHUNK_BANKS) * BANK
+                pieces.append(
+                    (clamped[:, o : o + BANK], backs[b, tau][:].rearrange("p a j -> p (a j)"))
+                )
+            for i, (after, before) in enumerate(pieces):
+                nc.vector.tensor_scalar(
+                    out=after,
+                    in0=before,
+                    scalar1=neg_zeta[:, tau : tau + 1],
+                    scalar2=None,
+                    op0=ALU.max,
+                    op1=ALU.min,
+                    accum_out=flip_lows[:, tau, i : i + 1],
+                )
+                if i == 0 and tau > 0:
+                    join_lows(tau - 1)
+
+        def join_lows(tau):
+            nc.vector.tensor_reduce(
+                out=low[:, column_of(last, tau)], in_=flip_lows[:, tau, :], axis=AXIS_X, op=ALU.min
+            )
+            scale_low(last, tau)
+
         def column_of(k, tau):
             return slice(tau * N_CHUNKS + k, tau * N_CHUNKS + k + 1)
 
@@ -346,6 +437,9 @@ def tile_kernelloglikelihood_kernel(
                 op1=ALU.min,
                 accum_out=low[:, column_of(k, tau)],
             )
+            scale_low(k, tau)
+
+        def scale_low(k, tau):
             nc.gpsimd.tensor_scalar(
                 out=low_s[:, column_of(k, tau)],
                 in0=low[:, column_of(k, tau)],
@@ -395,6 +489,9 @@ def tile_kernelloglikelihood_kernel(
 
         project(0)
         turn_x(1)
+        def is_plain(b):
+            return 0 <= b < FLIP_FROM
+
         def is_row_tile(tau):
             return 0 <= tau < ROW_TILES
 
@@ -422,24 +519,37 @@ def tile_kernelloglikelihood_kernel(
             if is_row_tile(n):
                 norm_z(n)
 
-            if is_bank(s):
+            if is_plain(s):
                 distances(s)
-            if is_bank(s + 1):
+            if is_plain(s + 1):
                 products(s + 1)
-            if is_bank(s - CHUNK_BANKS + 1):
+            if is_row_tile(s - N_BANKS + 2):
+                flip_back(s - N_BANKS + 2)
+            if is_row_tile(s - N_BANKS + 1):
+                clamp_flipped(s - N_BANKS + 1)
+                if s - N_BANKS + 1 == ROW_TILES - 1:
+                    join_lows(ROW_TILES - 1)
+            elif is_bank(s - CHUNK_BANKS + 1):
                 clamp_and_min(
                     (s - CHUNK_BANKS + 1) // ROW_TILES, (s - CHUNK_BANKS + 1) % ROW_TILES
                 )
             if is_bank(s + LEAD - 1):
                 regroup(s + LEAD - 1)
-            if is_bank(s + 2):
+            if is_plain(s + 2):
                 settle(s + 2)
+            if is_bank(s + FD) and s + FD >= FLIP_FROM:
+                join_norms(s + FD)
+                for part in (range(0, 2), range(2, 4)):
+                    flip(s + FD, part)
+                    flat_distances(s + FD, part)
             if is_bank(s + LEAD - 2):
                 quantise(s + LEAD - 2)
                 squares_on_pool(s + LEAD - 2)
             if is_bank(s - CHUNK_BANKS):
                 exponentials((s - CHUNK_BANKS) // ROW_TILES, (s - CHUNK_BANKS) % ROW_TILES)
-            if is_bank(s + 3):
+            if is_bank(s + 3) and s + 3 >= FLIP_FROM:
+                flip_norms(s + 3)
+            if is_plain(s + 3):
                 spread(s + 3)
             if is_bank(s + LEAD):
                 turn(s + LEAD)

@@ -281,12 +281,6 @@ def tile_kernelloglikelihood_kernel(
 
         def spread(b):
             spread_norms = psum_spread.tile([P, REF_TILES, P], F32, tag="spread")
-            for a in range(scalar_tiles(b)):
-                nc.tensor.transpose(
-                    spread_norms[:, a, :],
-                    banks[b]["norm_cols"][:, a : a + 1].to_broadcast([P, P]),
-                    ident_f32[:],
-                )
             if scalar_tiles(b) < REF_TILES:
                 for t in range(PACK):
                     nc.tensor.matmul(
@@ -296,6 +290,12 @@ def tile_kernelloglikelihood_kernel(
                         start=(t == 0),
                         stop=(t == PACK - 1),
                     )
+            for a in range(scalar_tiles(b)):
+                nc.tensor.transpose(
+                    spread_norms[:, a, :],
+                    banks[b]["norm_cols"][:, a : a + 1].to_broadcast([P, P]),
+                    ident_f32[:],
+                )
             banks[b]["spread"] = spread_norms
 
         def settle(b):

import math
from contextlib import ExitStack

import concourse.masks as masks
import concourse.mybir as mybir

F32 = mybir.dt.float32
BF16 = mybir.dt.bfloat16
I32 = mybir.dt.int32
U32 = mybir.dt.uint32
U8 = mybir.dt.uint8
FP8X4 = mybir.dt.float8_e4m3fn_x4
ALU = mybir.AluOpType
ACT = mybir.ActivationFunctionType
AXIS_X = mybir.AxisListType.X

P = 128
PACK = 4
K_PASS = P * PACK
BANK = 512

B, D, DC, NREF = 512, 1024, 512, 16384
ROW_TILES = B // P
X_PASSES = D // K_PASS
N_BANKS = NREF // BANK
REF_TILES = BANK // P
CHUNK_BANKS = 4
CHUNK = CHUNK_BANKS * BANK
N_CHUNKS = N_BANKS // CHUNK_BANKS
LEAD = 6
LOADS_AHEAD = 4

HALF_ROOT = math.sqrt(0.5)
FLIP_FROM = 30
FLIP_BANKS = N_BANKS - FLIP_FROM
FD = 2
POOL_FROM = 6
VECTOR_SETTLES = 4
POOL_TILES = 2

FLOPS = 2 * B * D * DC + 2 * B * DC * NREF


def tile_kernelloglikelihood_kernel(
    tc, x, pca_weight_words, pca_weight_scales, pca_bias, X_ref, bandwidth, out
):
    nc = tc.nc
    with ExitStack() as ctx:
        keep = ctx.enter_context(tc.tile_pool(name="keep", bufs=1))
        rows_pool = ctx.enter_context(tc.tile_pool(name="rows", bufs=LOADS_AHEAD + 2))
        grouped_pool = ctx.enter_context(tc.tile_pool(name="grouped", bufs=4))
        flat_pool = ctx.enter_context(tc.tile_pool(name="flat", bufs=FLIP_BANKS * REF_TILES))
        square_pool = ctx.enter_context(tc.tile_pool(name="square", bufs=3))
        bank_pool = ctx.enter_context(tc.tile_pool(name="bank", bufs=LEAD + 1))
        dist_pool = ctx.enter_context(tc.tile_pool(name="dist", bufs=2 * ROW_TILES))
        junk_pool = ctx.enter_context(tc.tile_pool(name="junk", bufs=2))
        psum_turn = ctx.enter_context(tc.psum_pool(name="psum_turn", bufs=2))
        psum_spread = ctx.enter_context(tc.psum_pool(name="psum_spread", bufs=2))
        psum_prod = ctx.enter_context(tc.psum_pool(name="psum_prod", bufs=4))
        ctx.enter_context(tc.manual_schedule())

        w_scales = keep.tile([P, X_PASSES, DC], U8, align_bytes=64)
        nc.vector.memset(w_scales[:].rearrange("p g n -> p (g n)").bitcast(I32), 0)
        bias_row = keep.tile([P, DC], BF16)
        nc.vector.memset(bias_row[:].bitcast(I32), 0)
        h_row = keep.tile([P, 2], BF16)
        nc.vector.memset(h_row[:].bitcast(I32), 0)
        ones = keep.tile([P, P], BF16)
        nc.vector.memset(ones[:], 1.0)

        x_rows = keep.tile([P, ROW_TILES, D], BF16)
        w_codes = keep.tile([P, X_PASSES, DC], U32, align_bytes=64)
        banks = {}

        def load_x(tau):
            nc.sync.dma_start(out=x_rows[:, tau, :], in_=x[tau * P : (tau + 1) * P, :])

        def load_bank(b):
            rows = rows_pool.tile([P, REF_TILES, DC], BF16, tag="rows")
            nc.sync.dma_start(
                out=rows[:],
                in_=X_ref[b * BANK : (b + 1) * BANK, :].rearrange("(p a) c -> p a c", a=REF_TILES),
            )
            banks[b] = {"rows": rows}

        load_x(0)
        for quadrant in range(4):
            nc.sync.dma_start(
                out=w_scales[32 * quadrant : 32 * quadrant + 4, :, :].bitcast(I32),
                in_=pca_weight_scales[:, 4 * quadrant : 4 * quadrant + 4, :]
                .rearrange("g r n -> r g n")
                .bitcast(I32),
            )
        for g in range(X_PASSES):
            nc.sync.dma_start(
                out=w_codes[:, g, :].bitcast(I32),
                in_=pca_weight_words[g].rearrange("p n t -> p (n t)").bitcast(I32),
            )
        nc.sync.dma_start(out=h_row[0:1, 0:1], in_=bandwidth.unsqueeze(0))
        nc.sync.dma_start(out=bias_row[0:1, :], in_=pca_bias.unsqueeze(0))
        for tau in range(1, ROW_TILES):
            load_x(tau)
            load_bank(tau - 1)
        load_bank(ROW_TILES - 1)
        assert LOADS_AHEAD == ROW_TILES

        half_f32 = keep.tile([P, P], F32)
        nc.gpsimd.memset(half_f32[:], 0.5)
        ident_f32 = keep.tile([P, P], F32)
        masks.make_identity(nc, ident_f32[:])
        ident_bf16 = keep.tile([P, P], BF16)
        masks.make_identity(nc, ident_bf16[:])

        x_words = x_rows[:].bitcast(F32)
        x_grouped = keep.tile([P, ROW_TILES, X_PASSES * P * PACK], BF16, align_bytes=64)
        x_codes = keep.tile([P, ROW_TILES, X_PASSES * P], U32, align_bytes=64)
        x_scales = keep.tile([P, ROW_TILES, X_PASSES * P], U8, align_bytes=64)
        z_f32 = keep.tile([P, ROW_TILES, DC], F32)
        z_planes = keep.tile([P, ROW_TILES, DC], BF16)
        z_grouped = keep.tile([P, ROW_TILES, P * PACK], BF16, align_bytes=64)
        z_codes = keep.tile([P, ROW_TILES, P], U32, align_bytes=64)
        z_scales = keep.tile([P, ROW_TILES, P], U8, align_bytes=64)
        neg_zeta = keep.tile([P, ROW_TILES], F32)

        x_turned_tiles, z_acc_tiles, z_turned_tiles = {}, {}, {}

        def turn_x(tau):
            x_turned = psum_prod.tile([P, X_PASSES, 2, P], F32, tag="prod")
            for g in range(X_PASSES):
                for u in range(2):
                    nc.tensor.transpose(
                        x_turned[:, g, u, :],
                        x_words[:, tau, 256 * g + u : 256 * (g + 1) : 2],
                        ident_f32[:],
                    )
            x_turned_tiles[tau] = x_turned

        def regroup_x(tau):
            x_turned = x_turned_tiles[tau]
            nc.vector.tensor_copy(
                out=x_grouped[:, tau, :]
                .bitcast(F32)
                .rearrange("p (g i u) -> p g i u", g=X_PASSES, u=2),
                in_=x_turned[:].rearrange("p g u i -> p g i u"),
            )

        def quantise_x(tau):
            nc.vector.quantize_mx(
                out=x_codes[:, tau, :].bitcast(FP8X4),
                scales=x_scales[:, tau, :],
                in_=x_grouped[:, tau, :],
            )

        def project(tau):
            z_acc = psum_prod.tile([P, DC], F32, tag="prod")
            z_acc_tiles[tau] = z_acc
            for g in range(X_PASSES):
                nc.tensor.matmul_mx(
                    out=z_acc[:],
                    lhsT=x_codes[:, tau, g * P : (g + 1) * P].bitcast(FP8X4),
                    lhsT_scale=x_scales[:, tau, g * P : (g + 1) * P],
                    rhs=w_codes[:, g, :].bitcast(FP8X4),
                    rhs_scale=w_scales[:, g, :],
                    start=(g == 0),
                    stop=(g == X_PASSES - 1),
                )

        def add_bias(tau):
            nc.vector.tensor_tensor(
                out=z_f32[:, tau, :], in0=z_acc_tiles[tau][:], in1=bias_bc[:], op=ALU.add
            )

        def round_z(tau):
            nc.vector.tensor_copy(
                out=z_planes[:, tau, :].rearrange("i (u e p) -> i u e p", u=2, e=2),
                in_=z_f32[:, tau, :].rearrange("i (u p e) -> i u e p", u=2, e=2),
            )

        def norm_z(tau):
            z_products = junk_pool.tile([P, DC], F32, tag="z_products")
            nc.vector.scalar_tensor_tensor(
                out=z_products[:],
                in0=z_f32[:, tau, :],
                scalar=-0.5,
                in1=z_f32[:, tau, :],
                op0=ALU.mult,
                op1=ALU.mult,
                accum_out=neg_zeta[:, tau : tau + 1],
            )

        def turn_z(tau):
            z_turned = psum_prod.tile([P, PACK, P], BF16, tag="prod")
            for t in range(PACK):
                nc.tensor.transpose(
                    z_turned[:, t, :], z_planes[:, tau, t * P : (t + 1) * P], ident_bf16[:]
                )
            z_turned_tiles[tau] = z_turned

        def regroup_z(tau):
            z_turned = z_turned_tiles[tau]
            nc.vector.tensor_copy(
                out=z_grouped[:, tau, :].rearrange("p (i t) -> p i t", t=PACK),
                in_=z_turned[:].rearrange("p t i -> p i t"),
            )

        def quantise_z(tau):
            nc.vector.quantize_mx(
                out=z_codes[:, tau, :].bitcast(FP8X4),
                scales=z_scales[:, tau, :],
                in_=z_grouped[:, tau, :],
            )

        def is_bank(b):
            return 0 <= b < N_BANKS

        def turn(b):
            row_words = banks[b]["rows"][:].bitcast(F32)
            banks[b]["turned"] = []
            for pair in range(REF_TILES // 2):
                turned = psum_turn.tile([P, 2, 2, P], F32, tag="turned")
                for a2 in range(2):
                    for u in range(2):
                        nc.tensor.transpose(
                            turned[:, a2, u, :],
                            row_words[:, 2 * pair + a2, u * P : (u + 1) * P],
                            ident_f32[:],
                        )
                banks[b]["turned"].append(turned)

        def scalar_tiles(b):
            return REF_TILES - POOL_TILES if b >= POOL_FROM else REF_TILES

        def norms(b):
            norm_cols = bank_pool.tile([P, REF_TILES], F32, tag="norm_cols")
            for a in range(scalar_tiles(b)):
                squares = junk_pool.tile([P, DC], BF16, tag="squares")
                nc.scalar.activation(
                    out=squares[:],
                    in_=banks[b]["rows"][:, a, :],
                    func=ACT.Square,
                    scale=HALF_ROOT,
                    accum_out=norm_cols[:, a : a + 1],
                )
            banks[b]["norm_cols"] = norm_cols

        def regroup(b):
            grouped = grouped_pool.tile([P, BANK * PACK], BF16, tag="grouped", align_bytes=64)
            grouped_words = grouped[:].bitcast(F32).rearrange(
                "p (a j u) -> p a j u", a=REF_TILES, u=2
            )
            for pair in range(REF_TILES // 2):
                nc.scalar.copy(
                    out=grouped_words[:, 2 * pair : 2 * pair + 2, :, :],
                    in_=banks[b]["turned"][pair][:].rearrange("p a u j -> p a j u"),
                )
            banks[b]["grouped"] = grouped

        def quantise(b):
            codes = bank_pool.tile([P, BANK], U32, tag="codes", align_bytes=64)
            scales = bank_pool.tile([P, BANK], U8, tag="scales", align_bytes=64)
            nc.vector.quantize_mx(
                out=codes[:].bitcast(FP8X4), scales=scales[:], in_=banks[b]["grouped"][:]
            )
            banks[b]["codes"] = codes
            banks[b]["scales"] = scales

        def squares_on_pool(b):
            if scalar_tiles(b) == REF_TILES:
                return
            squares_t = square_pool.tile([P, PACK, POOL_TILES * P], F32, tag="squares_t")
            values = banks[b]["grouped"][:].rearrange("p (a j t) -> p a t j", a=REF_TILES, t=PACK)
            for a in range(POOL_TILES):
                tile_values = values[:, scalar_tiles(b) + a, :, :]
                nc.gpsimd.tensor_tensor(
                    out=squares_t[:, :, a * P : (a + 1) * P],
                    in0=tile_values,
                    in1=tile_values,
                    op=ALU.mult,
                )
            banks[b]["squares_t"] = squares_t

        def spread(b):
            spread_norms = psum_spread.tile([P, REF_TILES, P], F32, tag="spread")
            if scalar_tiles(b) < REF_TILES:
                for t in range(PACK):
                    nc.tensor.matmul(
                        out=spread_norms[:, scalar_tiles(b) :, :],
                        lhsT=half_f32[:],
                        rhs=banks[b]["squares_t"][:, t, :],
                        start=(t == 0),
                        stop=(t == PACK - 1),
                    )
            for a in range(scalar_tiles(b)):
                nc.tensor.transpose(
                    spread_norms[:, a, :],
                    banks[b]["norm_cols"][:, a : a + 1].to_broadcast([P, P]),
                    ident_f32[:],
                )
            banks[b]["spread"] = spread_norms

        def settle(b):
            norm_rows = bank_pool.tile([P, BANK], F32, tag="norm_rows")
            leave = nc.vector.tensor_copy if b < VECTOR_SETTLES else nc.scalar.copy
            leave(out=norm_rows[:], in_=banks[b]["spread"][:].rearrange("p a j -> p (a j)"))
            banks[b]["norm_rows"] = norm_rows

        low = keep.tile([P, ROW_TILES * N_CHUNKS], F32)
        low_s = keep.tile([P, ROW_TILES * N_CHUNKS], F32)
        mass = keep.tile([P, ROW_TILES * N_CHUNKS], F32)
        dists = {}

        def products(b):
            banks[b]["prod"] = []
            for tau in range(ROW_TILES):
                prod = psum_prod.tile([P, BANK], F32, tag="prod")
                nc.tensor.matmul_mx(
                    out=prod[:],
                    lhsT=z_codes[:, tau, :].bitcast(FP8X4),
                    lhsT_scale=z_scales[:, tau, :],
                    rhs=banks[b]["codes"][:].bitcast(FP8X4),
                    rhs_scale=banks[b]["scales"][:],
                    start=True,
                    stop=True,
                )
                banks[b]["prod"].append(prod)

        def distances(b):
            k = b // CHUNK_BANKS
            cols = slice((b % CHUNK_BANKS) * BANK, (b % CHUNK_BANKS + 1) * BANK)
            for tau in range(ROW_TILES):
                if b % CHUNK_BANKS == 0:
                    dists[k, tau] = dist_pool.tile([P, CHUNK], F32, tag="dist", name="dist")
                nc.vector.tensor_tensor(
                    out=dists[k, tau][:, cols],
                    in0=banks[b]["norm_rows"][:],
                    in1=banks[b]["prod"][tau][:],
                    op=ALU.subtract,
                )

        def flip(b, part):
            for a in part:
                flipped = psum_turn.tile([P, BANK], F32, tag="turned", name="flipped")
                nc.tensor.matmul_mx(
                    out=flipped[:],
                    lhsT=banks[b]["codes"][:, a * P : (a + 1) * P].bitcast(FP8X4),
                    lhsT_scale=banks[b]["scales"][:, a * P : (a + 1) * P],
                    rhs=z_codes[:].rearrange("p t i -> p (t i)").bitcast(FP8X4),
                    rhs_scale=z_scales[:].rearrange("p t i -> p (t i)"),
                    start=True,
                    stop=True,
                )
                banks[b]["flipped", a] = flipped

        def flip_norms(b):
            pool_norms = psum_spread.tile([P, POOL_TILES], F32, tag="spread", name="pool_norms")
            for a in range(POOL_TILES):
                for t in range(PACK):
                    nc.tensor.matmul(
                        out=pool_norms[:, a : a + 1],
                        lhsT=banks[b]["squares_t"][:, t, a * P : (a + 1) * P],
                        rhs=half_f32[:, 0:1],
                        start=(t == 0),
                        stop=(t == PACK - 1),
                    )
            banks[b]["pool_norms"] = pool_norms

        def join_norms(b):
            nc.scalar.copy(
                out=banks[b]["norm_cols"][:, scalar_tiles(b) :], in_=banks[b]["pool_norms"][:]
            )

        def flat_distances(b, part):
            for a in part:
                flat = flat_pool.tile([P, BANK], F32, tag="flat", name="flat")
                nc.scalar.activation(
                    out=flat[:],
                    in_=banks[b]["flipped", a][:],
                    func=ACT.Identity,
                    scale=-1.0,
                    bias=banks[b]["norm_cols"][:, a : a + 1],
                )
                banks[b]["flat", a] = flat

        flip_lows = keep.tile([P, ROW_TILES, FLIP_BANKS + 1], F32)
        last = N_BANKS // CHUNK_BANKS - 1
        plain_banks = CHUNK_BANKS - FLIP_BANKS
        backs = {}

        def flip_back(tau):
            for b in range(FLIP_FROM, N_BANKS):
                back = psum_prod.tile([P, REF_TILES, P], F32, tag="prod", name="back")
                for a in range(REF_TILES):
                    nc.tensor.transpose(
                        back[:, a, :],
                        banks[b]["flat", a][:, tau * P : (tau + 1) * P],
                        ident_f32[:],
                    )
                backs[b, tau] = back

        def clamp_flipped(tau):
            clamped = dists[last, tau]
            pieces = [(clamped[:, 0 : plain_banks * BANK], clamped[:, 0 : plain_banks * BANK])]
            for b in range(FLIP_FROM, N_BANKS):
                o = (b % CHUNK_BANKS) * BANK
                pieces.append(
                    (clamped[:, o : o + BANK], backs[b, tau][:].rearrange("p a j -> p (a j)"))
                )
            for i, (after, before) in enumerate(pieces):
                nc.vector.tensor_scalar(
                    out=after,
                    in0=before,
                    scalar1=neg_zeta[:, tau : tau + 1],
                    scalar2=None,
                    op0=ALU.max,
                    op1=ALU.min,
                    accum_out=flip_lows[:, tau, i : i + 1],
                )
                if i == 0 and tau > 0:
                    join_lows(tau - 1)

        def join_lows(tau):
            nc.vector.tensor_reduce(
                out=low[:, column_of(last, tau)], in_=flip_lows[:, tau, :], axis=AXIS_X, op=ALU.min
            )
            scale_low(last, tau)

        def column_of(k, tau):
            return slice(tau * N_CHUNKS + k, tau * N_CHUNKS + k + 1)

        def clamp_and_min(k, tau):
            nc.vector.tensor_scalar(
                out=dists[k, tau][:],
                in0=dists[k, tau][:],
                scalar1=neg_zeta[:, tau : tau + 1],
                scalar2=None,
                op0=ALU.max,
                op1=ALU.min,
                accum_out=low[:, column_of(k, tau)],
            )
            scale_low(k, tau)

        def scale_low(k, tau):
            nc.gpsimd.tensor_scalar(
                out=low_s[:, column_of(k, tau)],
                in0=low[:, column_of(k, tau)],
                scalar1=pos_s[:, 0:1],
                scalar2=0.0,
                op0=ALU.mult,
                op1=ALU.add,
            )

        def exponentials(k, tau):
            terms = junk_pool.tile([P, CHUNK], BF16, tag="terms")
            nc.scalar.activation(
                out=terms[:],
                in_=dists[k, tau][:],
                func=ACT.Exp,
                scale=neg_s[:, 0:1],
                bias=low_s[:, column_of(k, tau)],
                accum_out=mass[:, column_of(k, tau)],
            )

        turn_x(0)
        regroup_x(0)
        quantise_x(0)

        h = keep.tile([P, 1], F32)
        h_everywhere = psum_spread.tile([P, 2], F32, tag="spread")
        nc.tensor.matmul(out=h_everywhere[:], lhsT=ones[:], rhs=h_row[:], start=True, stop=True)
        nc.vector.tensor_copy(out=h[:], in_=h_everywhere[:, 0:1])
        bias_everywhere = psum_spread.tile([P, DC], F32, tag="spread")
        nc.tensor.matmul(
            out=bias_everywhere[:], lhsT=ones[:], rhs=bias_row[:], start=True, stop=True
        )
        bias_bc = keep.tile([P, DC], F32)
        nc.scalar.copy(out=bias_bc[:], in_=bias_everywhere[:])
        inv_h = keep.tile([P, 1], F32)
        nc.vector.reciprocal(out=inv_h[:], in_=h[:])
        neg_s = keep.tile([P, 1], F32)
        nc.vector.scalar_tensor_tensor(
            out=neg_s[:], in0=inv_h[:], scalar=-1.0, in1=inv_h[:], op0=ALU.mult, op1=ALU.mult
        )
        pos_s = keep.tile([P, 1], F32)
        nc.vector.tensor_scalar(
            out=pos_s[:], in0=neg_s[:], scalar1=-1.0, scalar2=None, op0=ALU.mult
        )
        log_h = keep.tile([P, 1], F32)
        nc.scalar.activation(out=log_h[:], in_=h[:], func=ACT.Ln)

        project(0)
        turn_x(1)
        def is_plain(b):
            return 0 <= b < FLIP_FROM

        def is_row_tile(tau):
            return 0 <= tau < ROW_TILES

        assert LEAD >= ROW_TILES + 2
        assert CHUNK_BANKS == ROW_TILES
        last_finish = N_BANKS - 1 + ROW_TILES
        for s in range(-LEAD, last_finish + 1):
            n = s + LEAD
            if is_row_tile(n + 1):
                regroup_x(n + 1)
            if is_row_tile(n):
                add_bias(n)
            if is_row_tile(n - 1):
                regroup_z(n - 1)
            if is_row_tile(n + 2):
                turn_x(n + 2)
            if is_row_tile(n + 1):
                quantise_x(n + 1)
            if is_row_tile(n):
                round_z(n)
            if is_row_tile(n + 1):
                project(n + 1)
            if is_row_tile(n - 1):
                quantise_z(n - 1)
            if is_row_tile(n):
                norm_z(n)

            if is_plain(s):
                distances(s)
            if is_plain(s + 1):
                products(s + 1)
            if is_row_tile(s - N_BANKS + 2):
                flip_back(s - N_BANKS + 2)
            if is_row_tile(s - N_BANKS + 1):
                clamp_flipped(s - N_BANKS + 1)
                if s - N_BANKS + 1 == ROW_TILES - 1:
                    join_lows(ROW_TILES - 1)
            elif is_bank(s - CHUNK_BANKS + 1):
                clamp_and_min(
                    (s - CHUNK_BANKS + 1) // ROW_TILES, (s - CHUNK_BANKS + 1) % ROW_TILES
                )
            if is_bank(s + LEAD - 1):
                regroup(s + LEAD - 1)
            if is_plain(s + 2):
                settle(s + 2)
            if is_bank(s + FD) and s + FD >= FLIP_FROM:
                join_norms(s + FD)
                for part in (range(0, 2), range(2, 4)):
                    flip(s + FD, part)
                    flat_distances(s + FD, part)
            if is_bank(s + LEAD - 2):
                quantise(s + LEAD - 2)
                squares_on_pool(s + LEAD - 2)
            if is_bank(s - CHUNK_BANKS):
                exponentials((s - CHUNK_BANKS) // ROW_TILES, (s - CHUNK_BANKS) % ROW_TILES)
            if is_bank(s + 3) and s + 3 >= FLIP_FROM:
                flip_norms(s + 3)
            if is_plain(s + 3):
                spread(s + 3)
            if is_bank(s + LEAD):
                turn(s + LEAD)
                norms(s + LEAD)
            if is_row_tile(n):
                turn_z(n)
            if is_bank(s + LEAD + LOADS_AHEAD):
                load_bank(s + LEAD + LOADS_AHEAD)

        by_tile = "p (t k) -> p t k"
        lowest = keep.tile([P, ROW_TILES], F32)
        nc.vector.tensor_reduce(
            out=lowest[:], in_=low[:].rearrange(by_tile, t=ROW_TILES), axis=AXIS_X, op=ALU.min
        )
        weight = keep.tile([P, ROW_TILES * N_CHUNKS], F32)
        nc.vector.tensor_tensor(
            out=weight[:].rearrange(by_tile, t=ROW_TILES),
            in0=low[:].rearrange(by_tile, t=ROW_TILES),
            in1=lowest[:].unsqueeze(2).to_broadcast([P, ROW_TILES, N_CHUNKS]),
            op=ALU.subtract,
        )
        nc.scalar.activation(out=weight[:], in_=weight[:], func=ACT.Exp, scale=neg_s[:, 0:1])
        constant = keep.tile([P, 1], F32)
        nc.vector.tensor_scalar(
            out=constant[:],
            in0=log_h[:],
            scalar1=-float(DC),
            scalar2=-math.log(NREF) - 0.5 * DC * math.log(2.0 * math.pi),
            op0=ALU.mult,
            op1=ALU.add,
        )
        offset = keep.tile([P, ROW_TILES], F32)
        nc.vector.tensor_tensor(out=offset[:], in0=neg_zeta[:], in1=lowest[:], op=ALU.subtract)
        nc.vector.tensor_scalar(
            out=offset[:],
            in0=offset[:],
            scalar1=pos_s[:, 0:1],
            scalar2=constant[:, 0:1],
            op0=ALU.mult,
            op1=ALU.add,
        )
        nc.vector.tensor_tensor(out=weight[:], in0=weight[:], in1=mass[:], op=ALU.mult)
        total = keep.tile([P, ROW_TILES], F32)
        nc.vector.tensor_reduce(
            out=total[:], in_=weight[:].rearrange(by_tile, t=ROW_TILES), axis=AXIS_X, op=ALU.add
        )
        log_total = keep.tile([P, ROW_TILES], F32)
        nc.scalar.activation(out=log_total[:], in_=total[:], func=ACT.Ln)
        result = keep.tile([P, P], F32)
        nc.gpsimd.memset(result[:], 0.0)
        nc.vector.tensor_tensor(
            out=result[:, 0:ROW_TILES], in0=log_total[:], in1=offset[:], op=ALU.add
        )
        result_turned = psum_turn.tile([P, P], F32, tag="turned")
        nc.tensor.transpose(result_turned[:], result[:], ident_f32[:])
        result_rows = keep.tile([P, P], F32)
        nc.vector.tensor_copy(out=result_rows[:], in_=result_turned[:])
        nc.sync.dma_start(
            out=out.rearrange("(t p) -> t p", p=P), in_=result_rows[0:ROW_TILES, :]
        )
